import numpy as np
import ml_dtypes


def mxq(x, axis, fmt="e4m3"):
    dtype, down = {"e4m3": (ml_dtypes.float8_e4m3fn, 7), "e5m2": (ml_dtypes.float8_e5m2, 14)}[fmt]
    v = np.moveaxis(np.asarray(x, np.float32).astype(ml_dtypes.bfloat16).astype(np.float64), axis, -1)
    blocks = v.reshape(v.shape[:-1] + (-1, 32))
    amax = np.abs(blocks).max(-1, keepdims=True)
    byte = np.maximum(np.where(amax > 0, np.frexp(amax)[1] - 1 + 127, 0) - down, 1)
    scale = np.exp2(byte - 127.0)
    codes = (blocks / scale).astype(np.float32).astype(dtype).astype(np.float64)
    return np.moveaxis((codes * scale).reshape(v.shape), -1, axis)


WIDE = False


def mx_kscale(k):
    if not WIDE:
        return np.ones(k)
    levels = np.array([10, -10, 5, -5, 0])
    a = np.random.permutation(np.resize(levels, k // 512 * 4)).reshape(k // 512, 4)
    idx = np.arange(k)
    return np.exp2(a[idx // 512, idx % 128 // 32])


BF16 = ml_dtypes.bfloat16


def bf(x):
    return np.asarray(x, np.float32).astype(BF16)


def f64(x):
    return np.asarray(x).astype(np.float64)


B, S, D, E, P = 1, 512, 1024, 1024, 16384
HALF = P // 2


def setup_inputs():
    s = mx_kscale(E)
    u = mx_kscale(HALF)
    pq = np.random.uniform(-np.pi, np.pi, (B, S, HALF))
    pk = np.random.uniform(-np.pi, np.pi, (B, S, HALF))
    return {
        "Q": bf(np.random.standard_normal((B, S, E)) * s),
        "K": bf(np.random.standard_normal((B, S, E)) / s),
        "V": bf(np.random.standard_normal((B, S, E)) * 2.0),
        "cos_q": bf(np.cos(pq) * u),
        "sin_q": bf(np.sin(pq) * u),
        "cos_k": bf(np.cos(pk) / u),
        "sin_k": bf(np.sin(pk) / u),
        "bifurcation_param": bf(1.0 + 0.1 * np.random.standard_normal(1)),
        "phase_coupling": bf(5.0 * (1.0 + 0.1 * np.random.standard_normal(1))),
    }


def reference(Q, K, V, cos_q, sin_q, cos_k, sin_k, bifurcation_param, phase_coupling):
    scores = (mxq(f64(Q), 2, "e4m3") @ mxq(f64(K), 2, "e4m3").transpose(0, 2, 1)) / np.sqrt(E)
    sync = ((mxq(f64(cos_q), 2, "e4m3") @ mxq(f64(cos_k), 2, "e4m3").transpose(0, 2, 1))
            + (mxq(f64(sin_q), 2, "e4m3") @ mxq(f64(sin_k), 2, "e4m3").transpose(0, 2, 1))) / HALF
    t = np.tanh(scores)
    bif = f64(bifurcation_param) * t * (1.0 - t)
    chaotic = scores + f64(phase_coupling) * sync + bif
    e = np.exp(chaotic - chaotic.max(-1, keepdims=True))
    return (mxq(e, 2, "e4m3") @ mxq(f64(V), 1, "e4m3")) / e.sum(-1, keepdims=True)

@@ -1,0 +1,313 @@
+from contextlib import ExitStack
+
+import concourse.mybir as mybir
+from concourse.masks import make_identity
+
+F32 = mybir.dt.float32
+BF16 = mybir.dt.bfloat16
+U32 = mybir.dt.uint32
+U8 = mybir.dt.uint8
+FP8X4 = mybir.dt.float8_e4m3fn_x4
+ALU = mybir.AluOpType
+ACT = mybir.ActivationFunctionType
+
+P = 128
+PACK = 4
+K_PASS = P * PACK
+S = 512
+TILES = S // P
+E = 1024
+HALF = 8192
+WIDTHS = (E, HALF, HALF)
+PAIR = 2
+PAIR_COLS = PAIR * K_PASS
+N_PAIRS = sum(WIDTHS) // PAIR_COLS
+CHUNK_COLS = 2048
+TOGETHER = 2
+ALONE_PAIRS = 4
+AHEAD = 2
+RAW_BUFS = 14
+VECTOR_EVERY = 4
+SCORE_SCALE = 1.0 / 32.0
+HALVES = 2
+
+FLOPS = 2 * S * S * (E + 2 * HALF) + 2 * S * S * E
+
+
+def tile_chaoticattentionmechanism_pb_k_kernel(
+    tc, Q, K, V, cos_q, sin_q, cos_k, sin_k, bifurcation_param, phase_coupling, out
+):
+    nc = tc.nc
+    with ExitStack() as ctx:
+        ctx.enter_context(tc.manual_schedule())
+        keep = ctx.enter_context(tc.tile_pool(name="keep", bufs=1))
+        raw_pool = ctx.enter_context(tc.tile_pool(name="raw_pool", bufs=RAW_BUFS))
+        stage = ctx.enter_context(tc.tile_pool(name="stage", bufs=2))
+        psum_work = ctx.enter_context(tc.psum_pool(name="psum_work", bufs=6))
+        psum_sync = ctx.enter_context(tc.psum_pool(name="psum_sync", bufs=TOGETHER))
+
+        query_rows = [
+            a.rearrange("b s k -> (b s) k").rearrange("(m p) k -> m p k", p=P) for a in (Q, cos_q, sin_q)
+        ]
+        key_rows = [
+            a.rearrange("b s k -> (b s) k").rearrange("(p t) k -> t p k", t=TILES) for a in (K, cos_k, sin_k)
+        ]
+        value_rows = V.rearrange("b s w -> (b s) w").rearrange("(p j) w -> p j w", j=PACK)
+        out_rows = out.rearrange("b s w -> (b s) w").rearrange("(m p) w -> m p w", p=P)
+
+        pairs = []
+        for array_index, width in enumerate(WIDTHS):
+            for col in range(0, width, PAIR_COLS):
+                pairs.append((array_index, col))
+
+        score_run = (0, [(m, 0) for m in range(TILES)])
+        stream = []
+        for pair in range(1, N_PAIRS):
+            stream.append((pair, [(m, pair) for m in range(TOGETHER)]))
+        for m in range(TOGETHER, TILES):
+            for first in range(1, N_PAIRS, ALONE_PAIRS):
+                stream.append((None, [(m, pair) for pair in range(first, first + ALONE_PAIRS)]))
+        values_step = N_PAIRS - 1
+
+        raw = {}
+        key_codes = {}
+        key_scales = {}
+        score_bank = {}
+        sync_bank = {}
+        base = {}
+        weights = {}
+        row_sum = {}
+        grouped_weights = {}
+        weight_codes = {}
+        weight_scales = {}
+        grouped_values = {}
+
+        def banks_of(run):
+            key_pair, query_banks = run
+            keys = [] if key_pair is None else [("key", t, key_pair) for t in range(TILES)]
+            return keys + [("query", m, pair) for m, pair in query_banks]
+
+        def load_run(run):
+            for side, row_tile, pair in banks_of(run):
+                array_index, col = pairs[pair]
+                chunk = col // CHUNK_COLS
+                if (side, row_tile, array_index, chunk) in raw:
+                    continue
+                width = min(CHUNK_COLS, WIDTHS[array_index])
+                rows = (key_rows if side == "key" else query_rows)[array_index][row_tile]
+                loaded = raw_pool.tile([P, width], BF16, tag="raw", name="loaded")
+                nc.sync.dma_start(out=loaded[:], in_=rows[:, chunk * CHUNK_COLS : chunk * CHUNK_COLS + width])
+                raw[(side, row_tile, array_index, chunk)] = loaded
+
+        def transpose_run(run):
+            key_pair, query_banks = run
+            n_keys = 0 if key_pair is None else TILES
+            grouped_keys = None
+            key_words = None
+            if key_pair is not None:
+                grouped_keys = stage.tile([P, PAIR * S * PACK], BF16, tag="grouped_wide", align_bytes=64)
+                key_words = grouped_keys[:].bitcast(F32).rearrange(
+                    "p (s t r u) -> p s t r u", s=PAIR, t=TILES, u=2
+                )
+            grouped_queries = stage.tile(
+                [P, len(query_banks) * PAIR * P * PACK], BF16, tag="grouped_queries", align_bytes=64
+            )
+            query_words = grouped_queries[:].bitcast(F32).rearrange(
+                "p (j s r u) -> p j s r u", j=len(query_banks), s=PAIR, u=2
+            )
+            for position, (side, row_tile, pair) in enumerate(banks_of(run)):
+                array_index, col = pairs[pair]
+                words = raw[(side, row_tile, array_index, col // CHUNK_COLS)][:].bitcast(F32)
+                first_word = (col % CHUNK_COLS) // 2
+                bank = psum_work.tile([P, PAIR, 2, P], F32, tag="work", name="bank")
+                for s in range(PAIR):
+                    for u in range(2):
+                        w0 = first_word + (2 * s + u) * P
+                        nc.tensor.transpose(bank[:, s, u, :], words[:, w0 : w0 + P], ident_f32[:])
+                dst = key_words[:, :, row_tile] if side == "key" else query_words[:, position - n_keys]
+                src = bank[:].rearrange("p s u r -> p s r u")
+                if position % VECTOR_EVERY == VECTOR_EVERY - 1:
+                    nc.vector.tensor_copy(out=dst, in_=src)
+                else:
+                    nc.scalar.copy(out=dst, in_=src)
+            return grouped_keys, grouped_queries
+
+        def quantise_run(run, grouped_keys, grouped_queries):
+            key_pair, query_banks = run
+            if key_pair is not None:
+                key_codes[key_pair] = keep.tile(
+                    [P, PAIR * S], U32, name="key_codes_%d" % key_pair, align_bytes=64
+                )
+                key_scales[key_pair] = keep.tile(
+                    [P, PAIR * S], U8, name="key_scales_%d" % key_pair, align_bytes=64
+                )
+                nc.vector.quantize_mx(
+                    out=key_codes[key_pair][:].bitcast(FP8X4), scales=key_scales[key_pair][:], in_=grouped_keys[:]
+                )
+            n_words = len(query_banks) * PAIR * P
+            query_codes = stage.tile([P, n_words], U32, tag="query_codes", align_bytes=64)
+            query_scales = stage.tile([P, n_words], U8, tag="query_scales", align_bytes=64)
+            nc.vector.quantize_mx(out=query_codes[:].bitcast(FP8X4), scales=query_scales[:], in_=grouped_queries[:])
+            return query_codes, query_scales
+
+        def multiply_run(run, query_codes, query_scales):
+            closed = []
+            for j, (m, pair) in enumerate(run[1]):
+                for s in range(PAIR):
+                    opens = pair <= 1 and s == 0
+                    closes = pair in (0, N_PAIRS - 1) and s == PAIR - 1
+                    if opens and pair == 0:
+                        score_bank[m] = psum_work.tile([P, S], F32, tag="work", name="score_bank")
+                    if opens and pair == 1:
+                        sync_bank[m] = psum_sync.tile([P, S], F32, tag="sync", name="sync_bank")
+                    query_cols = slice((j * PAIR + s) * P, (j * PAIR + s + 1) * P)
+                    key_cols = slice(s * S, (s + 1) * S)
+                    nc.tensor.matmul_mx(
+                        out=(score_bank if pair == 0 else sync_bank)[m][:],
+                        lhsT=query_codes[:, query_cols].bitcast(FP8X4),
+                        lhsT_scale=query_scales[:, query_cols],
+                        rhs=key_codes[pair][:, key_cols].bitcast(FP8X4),
+                        rhs_scale=key_scales[pair][:, key_cols],
+                        start=opens,
+                        stop=closes,
+                    )
+                    if closes and pair > 0:
+                        closed.append(m)
+            return closed
+
+        def bifurcate(m):
+            tanh = stage.tile([P, S], F32, tag="tanh")
+            nc.scalar.activation(out=tanh[:], in_=score_bank[m][:], func=ACT.Tanh, scale=SCORE_SCALE)
+            nc.vector.scalar_tensor_tensor(
+                out=tanh[:], in0=tanh[:], scalar=1.0, in1=tanh[:], op0=ALU.subtract, op1=ALU.mult
+            )
+            nc.vector.tensor_scalar(out=tanh[:], in0=tanh[:], scalar1=neg_bif[:, 0:1], scalar2=None, op0=ALU.mult)
+            base[m] = keep.tile([P, S], F32, name="base_%d" % m)
+            nc.vector.scalar_tensor_tensor(
+                out=base[m][:], in0=score_bank[m][:], scalar=SCORE_SCALE, in1=tanh[:], op0=ALU.mult, op1=ALU.add
+            )
+
+        def softmax_rows(m):
+            nc.vector.scalar_tensor_tensor(
+                out=base[m][:], in0=sync_bank[m][:], scalar=coupling[:, 0:1], in1=base[m][:], op0=ALU.mult, op1=ALU.add
+            )
+            neg_max = stage.tile([P, 1], F32, tag="neg_max")
+            nc.vector.tensor_reduce(out=neg_max[:], in_=base[m][:], axis=mybir.AxisListType.X, op=ALU.max, negate=True)
+            weights[m] = stage.tile([P, S], BF16, tag="weights", name="weights")
+            row_sum[m] = stage.tile([P, 1], F32, tag="row_sum", name="row_sum")
+            nc.scalar.activation(
+                out=weights[m][:], in_=base[m][:], func=ACT.Exp, bias=neg_max[:, 0:1], scale=1.0, accum_out=row_sum[m][:]
+            )
+
+        def transpose_weights(m):
+            flipped = psum_work.tile([P, TILES, P], BF16, tag="work", name="flipped")
+            for t in range(TILES):
+                nc.tensor.transpose(flipped[:, t, :], weights[m][:, t * P : (t + 1) * P], ident_bf16[:])
+            grouped_weights[m] = stage.tile([P, P, PACK], BF16, tag="grouped_weights", name="grouped_weights", align_bytes=64)
+            nc.scalar.copy(out=grouped_weights[m][:], in_=flipped[:].rearrange("p t q -> p q t"))
+
+        def quantise_weights(m):
+            weight_codes[m] = stage.tile([P, P], U32, tag="weight_codes", name="weight_codes", align_bytes=64)
+            weight_scales[m] = stage.tile([P, P], U8, tag="weight_scales", name="weight_scales", align_bytes=64)
+            nc.vector.quantize_mx(
+                out=weight_codes[m][:].bitcast(FP8X4),
+                scales=weight_scales[m][:],
+                in_=grouped_weights[m][:].rearrange("p q t -> p (q t)"),
+            )
+
+        def regroup_values(h):
+            grouped_values[h] = stage.tile([P, S, PACK], BF16, tag="grouped_wide", name="grouped_values", align_bytes=64)
+            nc.vector.tensor_copy(
+                out=grouped_values[h][:], in_=value_raw[:, :, h * S : (h + 1) * S].rearrange("p j w -> p w j")
+            )
+
+        def quantise_values(h):
+            nc.vector.quantize_mx(
+                out=value_codes[:, h * S : (h + 1) * S].bitcast(FP8X4),
+                scales=value_scales[:, h * S : (h + 1) * S],
+                in_=grouped_values[h][:].rearrange("p w j -> p (w j)"),
+            )
+
+        def weigh_values(m):
+            inv_sum = stage.tile([P, 1], F32, tag="inv_sum")
+            nc.vector.reciprocal(inv_sum[:], row_sum[m][:])
+            result = stage.tile([P, HALVES * S], F32, tag="result")
+            for h in range(HALVES):
+                product = psum_work.tile([P, S], F32, tag="work", name="product")
+                nc.tensor.matmul_mx(
+                    out=product[:],
+                    lhsT=weight_codes[m][:].bitcast(FP8X4),
+                    lhsT_scale=weight_scales[m][:],
+                    rhs=value_codes[:, h * S : (h + 1) * S].bitcast(FP8X4),
+                    rhs_scale=value_scales[:, h * S : (h + 1) * S],
+                    start=True,
+                    stop=True,
+                )
+                if h == 0:
+                    nc.scalar.activation(out=result[:, 0:S], in_=product[:], func=ACT.Copy, scale=inv_sum[:, 0:1])
+                else:
+                    nc.vector.tensor_scalar(
+                        out=result[:, S : 2 * S], in0=product[:], scalar1=inv_sum[:, 0:1], scalar2=None, op0=ALU.mult
+                    )
+            nc.sync.dma_start(out=out_rows[m], in_=result[:])
+
+        load_run(score_run)
+        for run in stream[:AHEAD]:
+            load_run(run)
+        bif_raw = keep.tile([P, 1], BF16)
+        nc.scalar.dma_start(out=bif_raw[:], in_=bifurcation_param.partition_broadcast(P))
+        coupling_raw = keep.tile([P, 1], BF16)
+        nc.scalar.dma_start(out=coupling_raw[:], in_=phase_coupling.partition_broadcast(P))
+        ident_f32 = keep.tile([P, P], F32)
+        make_identity(nc, ident_f32[:])
+        ident_bf16 = keep.tile([P, P], BF16)
+        make_identity(nc, ident_bf16[:])
+        warm = keep.tile([P, 1], F32)
+        nc.vector.memset(warm[:], 0.0)
+        nc.scalar.activation(out=warm[:], in_=warm[:], func=ACT.Exp)
+        value_raw = keep.tile([P, PACK, HALVES * S], BF16)
+        value_codes = keep.tile([P, HALVES * S], U32, align_bytes=64)
+        value_scales = keep.tile([P, HALVES * S], U8, align_bytes=64)
+
+        grouped = transpose_run(score_run)
+        codes = quantise_run(score_run, grouped[0], grouped[1])
+        multiply_run(score_run, codes[0], codes[1])
+        neg_bif = keep.tile([P, 1], F32)
+        nc.vector.tensor_scalar(out=neg_bif[:], in0=bif_raw[:], scalar1=-1.0, scalar2=None, op0=ALU.mult)
+        coupling = keep.tile([P, 1], F32)
+        nc.vector.tensor_scalar(out=coupling[:], in0=coupling_raw[:], scalar1=1.0 / HALF, scalar2=None, op0=ALU.mult)
+        for m in range(TILES):
+            bifurcate(m)
+
+        grouped = None
+        to_transpose = []
+        to_weigh = []
+        for step in range(len(stream) + 3):
+            if step + AHEAD < len(stream):
+                load_run(stream[step + AHEAD])
+            if step + AHEAD == values_step:
+                nc.sync.dma_start(out=value_raw[:], in_=value_rows)
+            codes = None
+            if 1 <= step <= len(stream):
+                codes = quantise_run(stream[step - 1], grouped[0], grouped[1])
+            for h in range(HALVES):
+                if step == values_step + h + 1:
+                    quantise_values(h)
+            for m in to_weigh:
+                quantise_weights(m)
+            if step < len(stream):
+                grouped = transpose_run(stream[step])
+            for m in to_transpose:
+                transpose_weights(m)
+            closed = []
+            if codes is not None:
+                closed = multiply_run(stream[step - 1], codes[0], codes[1])
+            for m in closed:
+                softmax_rows(m)
+            for m in to_weigh:
+                weigh_values(m)
+            for h in range(HALVES):
+                if step == values_step + h:
+                    regroup_values(h)
+            to_weigh = to_transpose
+            to_transpose = closed

@@ -27,7 +27,9 @@ TOGETHER = 2
 ALONE_PAIRS = 4
 AHEAD = 2
 RAW_BUFS = 14
-VECTOR_EVERY = 4
+SCALAR_BANKS = 5
+BIF_FIRST = 2
+BIF_EVERY = 3
 SCORE_SCALE = 1.0 / 32.0
 HALVES = 2
 
@@ -60,14 +62,13 @@ def tile_chaoticattentionmechanism_pb_k_kernel(
             for col in range(0, width, PAIR_COLS):
                 pairs.append((array_index, col))
 
-        score_run = (0, [(m, 0) for m in range(TILES)])
-        stream = []
+        stream = [(0, [(m, 0) for m in range(TILES)])]
         for pair in range(1, N_PAIRS):
             stream.append((pair, [(m, pair) for m in range(TOGETHER)]))
         for m in range(TOGETHER, TILES):
             for first in range(1, N_PAIRS, ALONE_PAIRS):
                 stream.append((None, [(m, pair) for pair in range(first, first + ALONE_PAIRS)]))
-        values_step = N_PAIRS - 1
+        values_step = N_PAIRS
 
         raw = {}
         key_codes = {}
@@ -126,10 +127,10 @@ def tile_chaoticattentionmechanism_pb_k_kernel(
                         nc.tensor.transpose(bank[:, s, u, :], words[:, w0 : w0 + P], ident_f32[:])
                 dst = key_words[:, :, row_tile] if side == "key" else query_words[:, position - n_keys]
                 src = bank[:].rearrange("p s u r -> p s r u")
-                if position % VECTOR_EVERY == VECTOR_EVERY - 1:
-                    nc.vector.tensor_copy(out=dst, in_=src)
-                else:
+                if position < SCALAR_BANKS:
                     nc.scalar.copy(out=dst, in_=src)
+                else:
+                    nc.vector.tensor_copy(out=dst, in_=src)
             return grouped_keys, grouped_queries
 
         def quantise_run(run, grouped_keys, grouped_queries):
@@ -171,20 +172,27 @@ def tile_chaoticattentionmechanism_pb_k_kernel(
                         start=opens,
                         stop=closes,
                     )
-                    if closes and pair > 0:
+                    if closes:
                         closed.append(m)
             return closed
 
+        def save_scores(m):
+            base[m] = keep.tile([P, S], F32, name="base_%d" % m)
+            if m % 2 == 0:
+                nc.scalar.activation(out=base[m][:], in_=score_bank[m][:], func=ACT.Copy, scale=SCORE_SCALE)
+            else:
+                nc.vector.tensor_scalar(
+                    out=base[m][:], in0=score_bank[m][:], scalar1=SCORE_SCALE, scalar2=None, op0=ALU.mult
+                )
+
         def bifurcate(m):
             tanh = stage.tile([P, S], F32, tag="tanh")
-            nc.scalar.activation(out=tanh[:], in_=score_bank[m][:], func=ACT.Tanh, scale=SCORE_SCALE)
+            nc.scalar.activation(out=tanh[:], in_=base[m][:], func=ACT.Tanh)
             nc.vector.scalar_tensor_tensor(
                 out=tanh[:], in0=tanh[:], scalar=1.0, in1=tanh[:], op0=ALU.subtract, op1=ALU.mult
             )
-            nc.vector.tensor_scalar(out=tanh[:], in0=tanh[:], scalar1=neg_bif[:, 0:1], scalar2=None, op0=ALU.mult)
-            base[m] = keep.tile([P, S], F32, name="base_%d" % m)
             nc.vector.scalar_tensor_tensor(
-                out=base[m][:], in0=score_bank[m][:], scalar=SCORE_SCALE, in1=tanh[:], op0=ALU.mult, op1=ALU.add
+                out=base[m][:], in0=tanh[:], scalar=neg_bif[:, 0:1], in1=base[m][:], op0=ALU.mult, op1=ALU.add
             )
 
         def softmax_rows(m):
@@ -251,7 +259,6 @@ def tile_chaoticattentionmechanism_pb_k_kernel(
                     )
             nc.sync.dma_start(out=out_rows[m], in_=result[:])
 
-        load_run(score_run)
         for run in stream[:AHEAD]:
             load_run(run)
         bif_raw = keep.tile([P, 1], BF16)
@@ -269,20 +276,14 @@ def tile_chaoticattentionmechanism_pb_k_kernel(
         value_codes = keep.tile([P, HALVES * S], U32, align_bytes=64)
         value_scales = keep.tile([P, HALVES * S], U8, align_bytes=64)
 
-        grouped = transpose_run(score_run)
-        codes = quantise_run(score_run, grouped[0], grouped[1])
-        multiply_run(score_run, codes[0], codes[1])
         neg_bif = keep.tile([P, 1], F32)
-        nc.vector.tensor_scalar(out=neg_bif[:], in0=bif_raw[:], scalar1=-1.0, scalar2=None, op0=ALU.mult)
         coupling = keep.tile([P, 1], F32)
-        nc.vector.tensor_scalar(out=coupling[:], in0=coupling_raw[:], scalar1=1.0 / HALF, scalar2=None, op0=ALU.mult)
-        for m in range(TILES):
-            bifurcate(m)
 
         grouped = None
         to_transpose = []
+        to_quantise = []
         to_weigh = []
-        for step in range(len(stream) + 3):
+        for step in range(len(stream) + 4):
             if step + AHEAD < len(stream):
                 load_run(stream[step + AHEAD])
             if step + AHEAD == values_step:
@@ -291,9 +292,9 @@ def tile_chaoticattentionmechanism_pb_k_kernel(
             if 1 <= step <= len(stream):
                 codes = quantise_run(stream[step - 1], grouped[0], grouped[1])
             for h in range(HALVES):
-                if step == values_step + h + 1:
+                if step == values_step + h + 2:
                     quantise_values(h)
-            for m in to_weigh:
+            for m in to_quantise:
                 quantise_weights(m)
             if step < len(stream):
                 grouped = transpose_run(stream[step])
@@ -302,12 +303,24 @@ def tile_chaoticattentionmechanism_pb_k_kernel(
             closed = []
             if codes is not None:
                 closed = multiply_run(stream[step - 1], codes[0], codes[1])
+            if step == 1:
+                for m in closed:
+                    save_scores(m)
+                closed = []
+                nc.vector.tensor_scalar(out=neg_bif[:], in0=bif_raw[:], scalar1=-1.0, scalar2=None, op0=ALU.mult)
+                nc.vector.tensor_scalar(
+                    out=coupling[:], in0=coupling_raw[:], scalar1=1.0 / HALF, scalar2=None, op0=ALU.mult
+                )
             for m in closed:
                 softmax_rows(m)
             for m in to_weigh:
                 weigh_values(m)
             for h in range(HALVES):
-                if step == values_step + h:
+                if step == values_step + h + 1:
                     regroup_values(h)
-            to_weigh = to_transpose
+            for m in range(TILES):
+                if step == BIF_FIRST + BIF_EVERY * m:
+                    bifurcate(m)
+            to_weigh = to_quantise
+            to_quantise = to_transpose
             to_transpose = closed

@@ -28,12 +28,16 @@ ALONE_PAIRS = 4
 AHEAD = 2
 RAW_BUFS = 14
 SCALAR_BANKS = 5
-BIF_FIRST = 2
-BIF_EVERY = 3
+MAX_BANKS = 4
+LAG = 2
 SCORE_SCALE = 1.0 / 32.0
 HALVES = 2
 
 FLOPS = 2 * S * S * (E + 2 * HALF) + 2 * S * S * E
+
+
+def portion(items, index, count):
+    return items[index * len(items) // count : (index + 1) * len(items) // count]
 
 
 def tile_chaoticattentionmechanism_pb_k_kernel(
@@ -62,13 +66,15 @@ def tile_chaoticattentionmechanism_pb_k_kernel(
             for col in range(0, width, PAIR_COLS):
                 pairs.append((array_index, col))
 
-        stream = [(0, [(m, 0) for m in range(TILES)])]
+        score_run = (0, [(m, 0) for m in range(TILES)])
+        stream = []
         for pair in range(1, N_PAIRS):
             stream.append((pair, [(m, pair) for m in range(TOGETHER)]))
         for m in range(TOGETHER, TILES):
             for first in range(1, N_PAIRS, ALONE_PAIRS):
                 stream.append((None, [(m, pair) for pair in range(first, first + ALONE_PAIRS)]))
-        values_step = N_PAIRS
+        first_alone = N_PAIRS - 1
+        values_step = first_alone - 1 + LAG
 
         raw = {}
         key_codes = {}
@@ -100,23 +106,28 @@ def tile_chaoticattentionmechanism_pb_k_kernel(
                 nc.sync.dma_start(out=loaded[:], in_=rows[:, chunk * CHUNK_COLS : chunk * CHUNK_COLS + width])
                 raw[(side, row_tile, array_index, chunk)] = loaded
 
-        def transpose_run(run):
+        def open_run(run):
             key_pair, query_banks = run
-            n_keys = 0 if key_pair is None else TILES
             grouped_keys = None
-            key_words = None
+            views = []
             if key_pair is not None:
                 grouped_keys = stage.tile([P, PAIR * S * PACK], BF16, tag="grouped_wide", align_bytes=64)
                 key_words = grouped_keys[:].bitcast(F32).rearrange(
                     "p (s t r u) -> p s t r u", s=PAIR, t=TILES, u=2
                 )
+                views = [key_words[:, :, t] for t in range(TILES)]
             grouped_queries = stage.tile(
                 [P, len(query_banks) * PAIR * P * PACK], BF16, tag="grouped_queries", align_bytes=64
             )
             query_words = grouped_queries[:].bitcast(F32).rearrange(
                 "p (j s r u) -> p j s r u", j=len(query_banks), s=PAIR, u=2
             )
-            for position, (side, row_tile, pair) in enumerate(banks_of(run)):
+            views = views + [query_words[:, j] for j in range(len(query_banks))]
+            return grouped_keys, grouped_queries, views
+
+        def transpose_banks(run, views, positions):
+            for position in positions:
+                side, row_tile, pair = banks_of(run)[position]
                 array_index, col = pairs[pair]
                 words = raw[(side, row_tile, array_index, col // CHUNK_COLS)][:].bitcast(F32)
                 first_word = (col % CHUNK_COLS) // 2
@@ -125,13 +136,10 @@ def tile_chaoticattentionmechanism_pb_k_kernel(
                     for u in range(2):
                         w0 = first_word + (2 * s + u) * P
                         nc.tensor.transpose(bank[:, s, u, :], words[:, w0 : w0 + P], ident_f32[:])
-                dst = key_words[:, :, row_tile] if side == "key" else query_words[:, position - n_keys]
-                src = bank[:].rearrange("p s u r -> p s r u")
                 if position < SCALAR_BANKS:
-                    nc.scalar.copy(out=dst, in_=src)
+                    nc.scalar.copy(out=views[position], in_=bank[:].rearrange("p s u r -> p s r u"))
                 else:
-                    nc.vector.tensor_copy(out=dst, in_=src)
-            return grouped_keys, grouped_queries
+                    nc.vector.tensor_copy(out=views[position], in_=bank[:].rearrange("p s u r -> p s r u"))
 
         def quantise_run(run, grouped_keys, grouped_queries):
             key_pair, query_banks = run
@@ -151,48 +159,43 @@ def tile_chaoticattentionmechanism_pb_k_kernel(
             nc.vector.quantize_mx(out=query_codes[:].bitcast(FP8X4), scales=query_scales[:], in_=grouped_queries[:])
             return query_codes, query_scales
 
-        def multiply_run(run, query_codes, query_scales):
-            closed = []
-            for j, (m, pair) in enumerate(run[1]):
-                for s in range(PAIR):
-                    opens = pair <= 1 and s == 0
-                    closes = pair in (0, N_PAIRS - 1) and s == PAIR - 1
-                    if opens and pair == 0:
-                        score_bank[m] = psum_work.tile([P, S], F32, tag="work", name="score_bank")
-                    if opens and pair == 1:
-                        sync_bank[m] = psum_sync.tile([P, S], F32, tag="sync", name="sync_bank")
-                    query_cols = slice((j * PAIR + s) * P, (j * PAIR + s + 1) * P)
-                    key_cols = slice(s * S, (s + 1) * S)
-                    nc.tensor.matmul_mx(
-                        out=(score_bank if pair == 0 else sync_bank)[m][:],
-                        lhsT=query_codes[:, query_cols].bitcast(FP8X4),
-                        lhsT_scale=query_scales[:, query_cols],
-                        rhs=key_codes[pair][:, key_cols].bitcast(FP8X4),
-                        rhs_scale=key_scales[pair][:, key_cols],
-                        start=opens,
-                        stop=closes,
-                    )
-                    if closes:
-                        closed.append(m)
-            return closed
+        def passes_of(run):
+            return [(j, m, pair, s) for j, (m, pair) in enumerate(run[1]) for s in range(PAIR)]
 
-        def save_scores(m):
-            base[m] = keep.tile([P, S], F32, name="base_%d" % m)
-            if m % 2 == 0:
-                nc.scalar.activation(out=base[m][:], in_=score_bank[m][:], func=ACT.Copy, scale=SCORE_SCALE)
-            else:
-                nc.vector.tensor_scalar(
-                    out=base[m][:], in0=score_bank[m][:], scalar1=SCORE_SCALE, scalar2=None, op0=ALU.mult
+        def multiply(passes, query_codes, query_scales):
+            closed = []
+            for j, m, pair, s in passes:
+                opens = pair <= 1 and s == 0
+                closes = pair in (0, N_PAIRS - 1) and s == PAIR - 1
+                if opens and pair == 0:
+                    score_bank[m] = psum_work.tile([P, S], F32, tag="work", name="score_bank")
+                if opens and pair == 1:
+                    sync_bank[m] = psum_sync.tile([P, S], F32, tag="sync", name="sync_bank")
+                query_cols = slice((j * PAIR + s) * P, (j * PAIR + s + 1) * P)
+                key_cols = slice(s * S, (s + 1) * S)
+                nc.tensor.matmul_mx(
+                    out=(score_bank if pair == 0 else sync_bank)[m][:],
+                    lhsT=query_codes[:, query_cols].bitcast(FP8X4),
+                    lhsT_scale=query_scales[:, query_cols],
+                    rhs=key_codes[pair][:, key_cols].bitcast(FP8X4),
+                    rhs_scale=key_scales[pair][:, key_cols],
+                    start=opens,
+                    stop=closes,
                 )
+                if closes and pair > 0:
+                    closed.append(m)
+            return closed
 
         def bifurcate(m):
             tanh = stage.tile([P, S], F32, tag="tanh")
-            nc.scalar.activation(out=tanh[:], in_=base[m][:], func=ACT.Tanh)
+            nc.scalar.activation(out=tanh[:], in_=score_bank[m][:], func=ACT.Tanh, scale=SCORE_SCALE)
             nc.vector.scalar_tensor_tensor(
                 out=tanh[:], in0=tanh[:], scalar=1.0, in1=tanh[:], op0=ALU.subtract, op1=ALU.mult
             )
+            nc.vector.tensor_scalar(out=tanh[:], in0=tanh[:], scalar1=neg_bif[:, 0:1], scalar2=None, op0=ALU.mult)
+            base[m] = keep.tile([P, S], F32, name="base_%d" % m)
             nc.vector.scalar_tensor_tensor(
-                out=base[m][:], in0=tanh[:], scalar=neg_bif[:, 0:1], in1=base[m][:], op0=ALU.mult, op1=ALU.add
+                out=base[m][:], in0=score_bank[m][:], scalar=SCORE_SCALE, in1=tanh[:], op0=ALU.mult, op1=ALU.add
             )
 
         def softmax_rows(m):
@@ -259,6 +262,7 @@ def tile_chaoticattentionmechanism_pb_k_kernel(
                     )
             nc.sync.dma_start(out=out_rows[m], in_=result[:])
 
+        load_run(score_run)
         for run in stream[:AHEAD]:
             load_run(run)
         bif_raw = keep.tile([P, 1], BF16)
@@ -276,41 +280,52 @@ def tile_chaoticattentionmechanism_pb_k_kernel(
         value_codes = keep.tile([P, HALVES * S], U32, align_bytes=64)
         value_scales = keep.tile([P, HALVES * S], U8, align_bytes=64)
 
+        opened = open_run(score_run)
+        transpose_banks(score_run, opened[2], range(len(opened[2])))
+        codes = quantise_run(score_run, opened[0], opened[1])
+        multiply(passes_of(score_run), codes[0], codes[1])
         neg_bif = keep.tile([P, 1], F32)
+        nc.vector.tensor_scalar(out=neg_bif[:], in0=bif_raw[:], scalar1=-1.0, scalar2=None, op0=ALU.mult)
         coupling = keep.tile([P, 1], F32)
+        nc.vector.tensor_scalar(out=coupling[:], in0=coupling_raw[:], scalar1=1.0 / HALF, scalar2=None, op0=ALU.mult)
+        for m in range(TILES):
+            bifurcate(m)
 
-        grouped = None
+        quantised = {}
         to_transpose = []
         to_quantise = []
         to_weigh = []
-        for step in range(len(stream) + 4):
+        for step in range(len(stream) + LAG + 3):
             if step + AHEAD < len(stream):
                 load_run(stream[step + AHEAD])
-            if step + AHEAD == values_step:
+            if step + AHEAD == first_alone:
                 nc.sync.dma_start(out=value_raw[:], in_=value_rows)
-            codes = None
             if 1 <= step <= len(stream):
-                codes = quantise_run(stream[step - 1], grouped[0], grouped[1])
+                quantised[step - 1] = quantise_run(stream[step - 1], opened[0], opened[1])
             for h in range(HALVES):
                 if step == values_step + h + 2:
                     quantise_values(h)
             for m in to_quantise:
                 quantise_weights(m)
+            positions = []
+            passes = []
             if step < len(stream):
-                grouped = transpose_run(stream[step])
-            for m in to_transpose:
-                transpose_weights(m)
+                opened = open_run(stream[step])
+                positions = list(range(len(opened[2])))
+            if LAG <= step < len(stream) + LAG:
+                passes = passes_of(stream[step - LAG])
+            n_portions = max(1, -(-len(positions) // MAX_BANKS))
             closed = []
-            if codes is not None:
-                closed = multiply_run(stream[step - 1], codes[0], codes[1])
-            if step == 1:
-                for m in closed:
-                    save_scores(m)
-                closed = []
-                nc.vector.tensor_scalar(out=neg_bif[:], in0=bif_raw[:], scalar1=-1.0, scalar2=None, op0=ALU.mult)
-                nc.vector.tensor_scalar(
-                    out=coupling[:], in0=coupling_raw[:], scalar1=1.0 / HALF, scalar2=None, op0=ALU.mult
-                )
+            for index in range(n_portions):
+                if positions:
+                    transpose_banks(stream[step], opened[2], portion(positions, index, n_portions))
+                if index == n_portions - 1:
+                    for m in to_transpose:
+                        transpose_weights(m)
+                if passes:
+                    closed.extend(
+                        multiply(portion(passes, index, n_portions), quantised[step - LAG][0], quantised[step - LAG][1])
+                    )
             for m in closed:
                 softmax_rows(m)
             for m in to_weigh:
@@ -318,9 +333,6 @@ def tile_chaoticattentionmechanism_pb_k_kernel(
             for h in range(HALVES):
                 if step == values_step + h + 1:
                     regroup_values(h)
-            for m in range(TILES):
-                if step == BIF_FIRST + BIF_EVERY * m:
-                    bifurcate(m)
             to_weigh = to_quantise
             to_quantise = to_transpose
             to_transpose = closed

@@ -22,22 +22,22 @@ WIDTHS = (E, HALF, HALF)
 PAIR = 2
 PAIR_COLS = PAIR * K_PASS
 N_PAIRS = sum(WIDTHS) // PAIR_COLS
-CHUNK_COLS = 2048
-TOGETHER = 2
-ALONE_PAIRS = 4
-AHEAD = 2
-RAW_BUFS = 14
-SCALAR_BANKS = 5
-MAX_BANKS = 4
-LAG = 2
+UNIT = 4
+LATE_PAIRS = UNIT
+FIRST_LATE = N_PAIRS - LATE_PAIRS
+KEYS_EVERY = 3
+AHEAD = 3
+RAW_BUFS = 2 * (AHEAD + 1)
+EMPTY_BOTH = "SVSVSSVS"
+EMPTY_KEYS = "SVSV"
+EMPTY_LATE = "SSVS"
 SCORE_SCALE = 1.0 / 32.0
 HALVES = 2
+VALUE_PARTS = 4
+VALUE_COLS = E // VALUE_PARTS
+VALUE_STEP = 6
 
 FLOPS = 2 * S * S * (E + 2 * HALF) + 2 * S * S * E
-
-
-def portion(items, index, count):
-    return items[index * len(items) // count : (index + 1) * len(items) // count]
 
 
 def tile_chaoticattentionmechanism_pb_k_kernel(
@@ -49,14 +49,14 @@ def tile_chaoticattentionmechanism_pb_k_kernel(
         keep = ctx.enter_context(tc.tile_pool(name="keep", bufs=1))
         raw_pool = ctx.enter_context(tc.tile_pool(name="raw_pool", bufs=RAW_BUFS))
         stage = ctx.enter_context(tc.tile_pool(name="stage", bufs=2))
-        psum_work = ctx.enter_context(tc.psum_pool(name="psum_work", bufs=6))
-        psum_sync = ctx.enter_context(tc.psum_pool(name="psum_sync", bufs=TOGETHER))
+        psum_work = ctx.enter_context(tc.psum_pool(name="psum_work", bufs=4))
+        psum_sync = ctx.enter_context(tc.psum_pool(name="psum_sync", bufs=TILES))
 
         query_rows = [
-            a.rearrange("b s k -> (b s) k").rearrange("(m p) k -> m p k", p=P) for a in (Q, cos_q, sin_q)
+            a.rearrange("b s k -> (b s) k").rearrange("(m p) k -> p m k", p=P) for a in (Q, cos_q, sin_q)
         ]
         key_rows = [
-            a.rearrange("b s k -> (b s) k").rearrange("(p t) k -> t p k", t=TILES) for a in (K, cos_k, sin_k)
+            a.rearrange("b s k -> (b s) k").rearrange("(p t) k -> p t k", t=TILES) for a in (K, cos_k, sin_k)
         ]
         value_rows = V.rearrange("b s w -> (b s) w").rearrange("(p j) w -> p j w", j=PACK)
         out_rows = out.rearrange("b s w -> (b s) w").rearrange("(m p) w -> m p w", p=P)
@@ -66,21 +66,24 @@ def tile_chaoticattentionmechanism_pb_k_kernel(
             for col in range(0, width, PAIR_COLS):
                 pairs.append((array_index, col))
 
-        score_run = (0, [(m, 0) for m in range(TILES)])
-        stream = []
-        for pair in range(1, N_PAIRS):
-            stream.append((pair, [(m, pair) for m in range(TOGETHER)]))
-        for m in range(TOGETHER, TILES):
-            for first in range(1, N_PAIRS, ALONE_PAIRS):
-                stream.append((None, [(m, pair) for pair in range(first, first + ALONE_PAIRS)]))
-        first_alone = N_PAIRS - 1
-        values_step = first_alone - 1 + LAG
+        steps = []
+        late = FIRST_LATE
+        for pair in range(FIRST_LATE):
+            steps.append((pair, [(m, pair) for m in range(TILES)]))
+            if pair % KEYS_EVERY == KEYS_EVERY - 1 and late < N_PAIRS:
+                steps.append((late, []))
+                late += 1
+        for m in range(TILES):
+            steps.append((None, [(m, pair) for pair in range(FIRST_LATE, N_PAIRS)]))
 
         raw = {}
         key_codes = {}
         key_scales = {}
+        query_codes = {}
+        query_scales = {}
         score_bank = {}
         sync_bank = {}
+        tanh = {}
         base = {}
         weights = {}
         row_sum = {}
@@ -89,60 +92,61 @@ def tile_chaoticattentionmechanism_pb_k_kernel(
         weight_scales = {}
         grouped_values = {}
 
-        def banks_of(run):
-            key_pair, query_banks = run
-            keys = [] if key_pair is None else [("key", t, key_pair) for t in range(TILES)]
-            return keys + [("query", m, pair) for m, pair in query_banks]
+        def new_raw():
+            return raw_pool.tile([P, UNIT, PAIR_COLS], BF16, tag="raw", name="loaded")
 
-        def load_run(run):
-            for side, row_tile, pair in banks_of(run):
-                array_index, col = pairs[pair]
-                chunk = col // CHUNK_COLS
-                if (side, row_tile, array_index, chunk) in raw:
-                    continue
-                width = min(CHUNK_COLS, WIDTHS[array_index])
-                rows = (key_rows if side == "key" else query_rows)[array_index][row_tile]
-                loaded = raw_pool.tile([P, width], BF16, tag="raw", name="loaded")
-                nc.sync.dma_start(out=loaded[:], in_=rows[:, chunk * CHUNK_COLS : chunk * CHUNK_COLS + width])
-                raw[(side, row_tile, array_index, chunk)] = loaded
-
-        def open_run(run):
-            key_pair, query_banks = run
-            grouped_keys = None
-            views = []
+        def load_step(i, pieces):
+            key_pair, queries = steps[i]
             if key_pair is not None:
-                grouped_keys = stage.tile([P, PAIR * S * PACK], BF16, tag="grouped_wide", align_bytes=64)
-                key_words = grouped_keys[:].bitcast(F32).rearrange(
-                    "p (s t r u) -> p s t r u", s=PAIR, t=TILES, u=2
-                )
-                views = [key_words[:, :, t] for t in range(TILES)]
-            grouped_queries = stage.tile(
-                [P, len(query_banks) * PAIR * P * PACK], BF16, tag="grouped_queries", align_bytes=64
-            )
-            query_words = grouped_queries[:].bitcast(F32).rearrange(
-                "p (j s r u) -> p j s r u", j=len(query_banks), s=PAIR, u=2
-            )
-            views = views + [query_words[:, j] for j in range(len(query_banks))]
-            return grouped_keys, grouped_queries, views
-
-        def transpose_banks(run, views, positions):
-            for position in positions:
-                side, row_tile, pair = banks_of(run)[position]
+                array_index, col = pairs[key_pair]
+                raw[(i, "key")] = new_raw()
+                for c in range(0, UNIT, UNIT // pieces):
+                    nc.sync.dma_start(
+                        out=raw[(i, "key")][:, c : c + UNIT // pieces, :],
+                        in_=key_rows[array_index][:, c : c + UNIT // pieces, col : col + PAIR_COLS],
+                    )
+            if queries:
+                m, pair = queries[0]
                 array_index, col = pairs[pair]
-                words = raw[(side, row_tile, array_index, col // CHUNK_COLS)][:].bitcast(F32)
-                first_word = (col % CHUNK_COLS) // 2
+                raw[(i, "query")] = new_raw()
+                if key_pair is not None:
+                    source = query_rows[array_index][:, :, col : col + PAIR_COLS]
+                else:
+                    source = query_rows[array_index][:, m, col : col + UNIT * PAIR_COLS].rearrange(
+                        "p (j k) -> p j k", j=UNIT
+                    )
+                for c in range(0, UNIT, UNIT // pieces):
+                    nc.sync.dma_start(
+                        out=raw[(i, "query")][:, c : c + UNIT // pieces, :], in_=source[:, c : c + UNIT // pieces, :]
+                    )
+
+        def transpose_unit(loaded, views, engines):
+            words = loaded[:].bitcast(F32)
+            for c in range(UNIT):
                 bank = psum_work.tile([P, PAIR, 2, P], F32, tag="work", name="bank")
                 for s in range(PAIR):
                     for u in range(2):
-                        w0 = first_word + (2 * s + u) * P
-                        nc.tensor.transpose(bank[:, s, u, :], words[:, w0 : w0 + P], ident_f32[:])
-                if position < SCALAR_BANKS:
-                    nc.scalar.copy(out=views[position], in_=bank[:].rearrange("p s u r -> p s r u"))
+                        w0 = (2 * s + u) * P
+                        nc.tensor.transpose(bank[:, s, u, :], words[:, c, w0 : w0 + P], ident_f32[:])
+                if engines[c] == "S":
+                    nc.scalar.copy(out=views[c], in_=bank[:].rearrange("p s u r -> p s r u"))
                 else:
-                    nc.vector.tensor_copy(out=views[position], in_=bank[:].rearrange("p s u r -> p s r u"))
+                    nc.vector.tensor_copy(out=views[c], in_=bank[:].rearrange("p s u r -> p s r u"))
 
-        def quantise_run(run, grouped_keys, grouped_queries):
-            key_pair, query_banks = run
+        def transpose_step(i):
+            key_pair, queries = steps[i]
+            grouped_keys = None
+            grouped_queries = None
+            if key_pair is not None:
+                grouped_keys = stage.tile([P, PAIR * S * PACK], BF16, tag="grouped_keys", align_bytes=64)
+                words = grouped_keys[:].bitcast(F32).rearrange("p (s t r u) -> p s t r u", s=PAIR, t=TILES, u=2)
+                engines = EMPTY_BOTH if queries else EMPTY_KEYS
+                transpose_unit(raw[(i, "key")], [words[:, :, t] for t in range(TILES)], engines)
+            if queries:
+                grouped_queries = stage.tile([P, UNIT * PAIR * P * PACK], BF16, tag="grouped_queries", align_bytes=64)
+                words = grouped_queries[:].bitcast(F32).rearrange("p (j s r u) -> p j s r u", j=UNIT, s=PAIR, u=2)
+                engines = EMPTY_LATE if key_pair is None else EMPTY_BOTH[UNIT:]
+                transpose_unit(raw[(i, "query")], [words[:, j] for j in range(UNIT)], engines)
             if key_pair is not None:
                 key_codes[key_pair] = keep.tile(
                     [P, PAIR * S], U32, name="key_codes_%d" % key_pair, align_bytes=64
@@ -153,49 +157,53 @@ def tile_chaoticattentionmechanism_pb_k_kernel(
                 nc.vector.quantize_mx(
                     out=key_codes[key_pair][:].bitcast(FP8X4), scales=key_scales[key_pair][:], in_=grouped_keys[:]
                 )
-            n_words = len(query_banks) * PAIR * P
-            query_codes = stage.tile([P, n_words], U32, tag="query_codes", align_bytes=64)
-            query_scales = stage.tile([P, n_words], U8, tag="query_scales", align_bytes=64)
-            nc.vector.quantize_mx(out=query_codes[:].bitcast(FP8X4), scales=query_scales[:], in_=grouped_queries[:])
-            return query_codes, query_scales
-
-        def passes_of(run):
-            return [(j, m, pair, s) for j, (m, pair) in enumerate(run[1]) for s in range(PAIR)]
-
-        def multiply(passes, query_codes, query_scales):
-            closed = []
-            for j, m, pair, s in passes:
-                opens = pair <= 1 and s == 0
-                closes = pair in (0, N_PAIRS - 1) and s == PAIR - 1
-                if opens and pair == 0:
-                    score_bank[m] = psum_work.tile([P, S], F32, tag="work", name="score_bank")
-                if opens and pair == 1:
-                    sync_bank[m] = psum_sync.tile([P, S], F32, tag="sync", name="sync_bank")
-                query_cols = slice((j * PAIR + s) * P, (j * PAIR + s + 1) * P)
-                key_cols = slice(s * S, (s + 1) * S)
-                nc.tensor.matmul_mx(
-                    out=(score_bank if pair == 0 else sync_bank)[m][:],
-                    lhsT=query_codes[:, query_cols].bitcast(FP8X4),
-                    lhsT_scale=query_scales[:, query_cols],
-                    rhs=key_codes[pair][:, key_cols].bitcast(FP8X4),
-                    rhs_scale=key_scales[pair][:, key_cols],
-                    start=opens,
-                    stop=closes,
+            if queries:
+                n_words = UNIT * PAIR * P
+                query_codes[i] = stage.tile([P, n_words], U32, tag="query_codes", name="codes", align_bytes=64)
+                query_scales[i] = stage.tile([P, n_words], U8, tag="query_scales", name="scales", align_bytes=64)
+                nc.vector.quantize_mx(
+                    out=query_codes[i][:].bitcast(FP8X4), scales=query_scales[i][:], in_=grouped_queries[:]
                 )
-                if closes and pair > 0:
-                    closed.append(m)
+
+        def multiply_step(i):
+            closed = []
+            for j, (m, pair) in enumerate(steps[i][1]):
+                for s in range(PAIR):
+                    opens = pair <= 1 and s == 0
+                    closes = pair in (0, N_PAIRS - 1) and s == PAIR - 1
+                    if opens and pair == 0:
+                        score_bank[m] = psum_sync.tile([P, S], F32, tag="sums", name="score_bank")
+                    if opens and pair == 1:
+                        sync_bank[m] = psum_sync.tile([P, S], F32, tag="sums", name="sync_bank")
+                    query_cols = slice((j * PAIR + s) * P, (j * PAIR + s + 1) * P)
+                    key_cols = slice(s * S, (s + 1) * S)
+                    nc.tensor.matmul_mx(
+                        out=(score_bank if pair == 0 else sync_bank)[m][:],
+                        lhsT=query_codes[i][:, query_cols].bitcast(FP8X4),
+                        lhsT_scale=query_scales[i][:, query_cols],
+                        rhs=key_codes[pair][:, key_cols].bitcast(FP8X4),
+                        rhs_scale=key_scales[pair][:, key_cols],
+                        start=opens,
+                        stop=closes,
+                    )
+                    if closes and pair > 0:
+                        closed.append(m)
             return closed
 
-        def bifurcate(m):
-            tanh = stage.tile([P, S], F32, tag="tanh")
-            nc.scalar.activation(out=tanh[:], in_=score_bank[m][:], func=ACT.Tanh, scale=SCORE_SCALE)
-            nc.vector.scalar_tensor_tensor(
-                out=tanh[:], in0=tanh[:], scalar=1.0, in1=tanh[:], op0=ALU.subtract, op1=ALU.mult
-            )
-            nc.vector.tensor_scalar(out=tanh[:], in0=tanh[:], scalar1=neg_bif[:, 0:1], scalar2=None, op0=ALU.mult)
+        def empty_scores(m):
+            tanh[m] = keep.tile([P, S], F32, name="tanh_%d" % m)
+            nc.scalar.activation(out=tanh[m][:], in_=score_bank[m][:], func=ACT.Tanh, scale=SCORE_SCALE)
             base[m] = keep.tile([P, S], F32, name="base_%d" % m)
+            nc.vector.tensor_scalar(
+                out=base[m][:], in0=score_bank[m][:], scalar1=SCORE_SCALE, scalar2=None, op0=ALU.mult
+            )
+
+        def bifurcate(m):
             nc.vector.scalar_tensor_tensor(
-                out=base[m][:], in0=score_bank[m][:], scalar=SCORE_SCALE, in1=tanh[:], op0=ALU.mult, op1=ALU.add
+                out=tanh[m][:], in0=tanh[m][:], scalar=1.0, in1=tanh[m][:], op0=ALU.subtract, op1=ALU.mult
+            )
+            nc.vector.scalar_tensor_tensor(
+                out=base[m][:], in0=tanh[m][:], scalar=neg_bif[:, 0:1], in1=base[m][:], op0=ALU.mult, op1=ALU.add
             )
 
         def softmax_rows(m):
@@ -205,7 +213,7 @@ def tile_chaoticattentionmechanism_pb_k_kernel(
             neg_max = stage.tile([P, 1], F32, tag="neg_max")
             nc.vector.tensor_reduce(out=neg_max[:], in_=base[m][:], axis=mybir.AxisListType.X, op=ALU.max, negate=True)
             weights[m] = stage.tile([P, S], BF16, tag="weights", name="weights")
-            row_sum[m] = stage.tile([P, 1], F32, tag="row_sum", name="row_sum")
+            row_sum[m] = keep.tile([P, 1], F32, name="row_sum_%d" % m)
             nc.scalar.activation(
                 out=weights[m][:], in_=base[m][:], func=ACT.Exp, bias=neg_max[:, 0:1], scale=1.0, accum_out=row_sum[m][:]
             )
@@ -226,17 +234,19 @@ def tile_chaoticattentionmechanism_pb_k_kernel(
                 in_=grouped_weights[m][:].rearrange("p q t -> p (q t)"),
             )
 
-        def regroup_values(h):
-            grouped_values[h] = stage.tile([P, S, PACK], BF16, tag="grouped_wide", name="grouped_values", align_bytes=64)
-            nc.vector.tensor_copy(
-                out=grouped_values[h][:], in_=value_raw[:, :, h * S : (h + 1) * S].rearrange("p j w -> p w j")
+        def regroup_values(part):
+            cols = slice(part * VALUE_COLS, (part + 1) * VALUE_COLS)
+            grouped_values[part] = stage.tile(
+                [P, VALUE_COLS, PACK], BF16, tag="grouped_values", name="grouped_values", align_bytes=64
             )
+            nc.scalar.copy(out=grouped_values[part][:], in_=raw["values"][:, :, cols].rearrange("p j w -> p w j"))
 
-        def quantise_values(h):
+        def quantise_values(part):
+            cols = slice(part * VALUE_COLS, (part + 1) * VALUE_COLS)
             nc.vector.quantize_mx(
-                out=value_codes[:, h * S : (h + 1) * S].bitcast(FP8X4),
-                scales=value_scales[:, h * S : (h + 1) * S],
-                in_=grouped_values[h][:].rearrange("p w j -> p (w j)"),
+                out=value_codes[:, cols].bitcast(FP8X4),
+                scales=value_scales[:, cols],
+                in_=grouped_values[part][:].rearrange("p w j -> p (w j)"),
             )
 
         def weigh_values(m):
@@ -260,11 +270,11 @@ def tile_chaoticattentionmechanism_pb_k_kernel(
                     nc.vector.tensor_scalar(
                         out=result[:, S : 2 * S], in0=product[:], scalar1=inv_sum[:, 0:1], scalar2=None, op0=ALU.mult
                     )
-            nc.sync.dma_start(out=out_rows[m], in_=result[:])
+                nc.sync.dma_start(out=out_rows[m][:, h * S : (h + 1) * S], in_=result[:, h * S : (h + 1) * S])
 
-        load_run(score_run)
-        for run in stream[:AHEAD]:
-            load_run(run)
+        load_step(0, UNIT)
+        for i in range(1, AHEAD):
+            load_step(i, 2)
         bif_raw = keep.tile([P, 1], BF16)
         nc.scalar.dma_start(out=bif_raw[:], in_=bifurcation_param.partition_broadcast(P))
         coupling_raw = keep.tile([P, 1], BF16)
@@ -276,63 +286,42 @@ def tile_chaoticattentionmechanism_pb_k_kernel(
         warm = keep.tile([P, 1], F32)
         nc.vector.memset(warm[:], 0.0)
         nc.scalar.activation(out=warm[:], in_=warm[:], func=ACT.Exp)
-        value_raw = keep.tile([P, PACK, HALVES * S], BF16)
-        value_codes = keep.tile([P, HALVES * S], U32, align_bytes=64)
-        value_scales = keep.tile([P, HALVES * S], U8, align_bytes=64)
-
-        opened = open_run(score_run)
-        transpose_banks(score_run, opened[2], range(len(opened[2])))
-        codes = quantise_run(score_run, opened[0], opened[1])
-        multiply(passes_of(score_run), codes[0], codes[1])
         neg_bif = keep.tile([P, 1], F32)
         nc.vector.tensor_scalar(out=neg_bif[:], in0=bif_raw[:], scalar1=-1.0, scalar2=None, op0=ALU.mult)
         coupling = keep.tile([P, 1], F32)
         nc.vector.tensor_scalar(out=coupling[:], in0=coupling_raw[:], scalar1=1.0 / HALF, scalar2=None, op0=ALU.mult)
-        for m in range(TILES):
-            bifurcate(m)
+        value_codes = keep.tile([P, E], U32, align_bytes=64)
+        value_scales = keep.tile([P, E], U8, align_bytes=64)
 
-        quantised = {}
         to_transpose = []
-        to_quantise = []
         to_weigh = []
-        for step in range(len(stream) + LAG + 3):
-            if step + AHEAD < len(stream):
-                load_run(stream[step + AHEAD])
-            if step + AHEAD == first_alone:
-                nc.sync.dma_start(out=value_raw[:], in_=value_rows)
-            if 1 <= step <= len(stream):
-                quantised[step - 1] = quantise_run(stream[step - 1], opened[0], opened[1])
-            for h in range(HALVES):
-                if step == values_step + h + 2:
-                    quantise_values(h)
-            for m in to_quantise:
+        for i in range(len(steps) + 3):
+            if i + AHEAD < len(steps):
+                load_step(i + AHEAD, 2)
+            if i == VALUE_STEP - AHEAD:
+                raw["values"] = new_raw()
+                nc.sync.dma_start(out=raw["values"][:], in_=value_rows)
+            if i < len(steps):
+                transpose_step(i)
+            for m in to_weigh:
                 quantise_weights(m)
-            positions = []
-            passes = []
-            if step < len(stream):
-                opened = open_run(stream[step])
-                positions = list(range(len(opened[2])))
-            if LAG <= step < len(stream) + LAG:
-                passes = passes_of(stream[step - LAG])
-            n_portions = max(1, -(-len(positions) // MAX_BANKS))
+                weigh_values(m)
             closed = []
-            for index in range(n_portions):
-                if positions:
-                    transpose_banks(stream[step], opened[2], portion(positions, index, n_portions))
-                if index == n_portions - 1:
-                    for m in to_transpose:
-                        transpose_weights(m)
-                if passes:
-                    closed.extend(
-                        multiply(portion(passes, index, n_portions), quantised[step - LAG][0], quantised[step - LAG][1])
-                    )
+            if 1 <= i <= len(steps):
+                closed = multiply_step(i - 1)
+            if i == 1:
+                for m in range(TILES):
+                    empty_scores(m)
+            if 2 <= i < 2 + TILES:
+                bifurcate(i - 2)
             for m in closed:
                 softmax_rows(m)
-            for m in to_weigh:
-                weigh_values(m)
-            for h in range(HALVES):
-                if step == values_step + h + 1:
-                    regroup_values(h)
-            to_weigh = to_quantise
-            to_quantise = to_transpose
+            for m in to_transpose:
+                transpose_weights(m)
+            for part in range(VALUE_PARTS):
+                if i == VALUE_STEP + part:
+                    regroup_values(part)
+                if i == VALUE_STEP + part + 1:
+                    quantise_values(part)
+            to_weigh = to_transpose
             to_transpose = closed

@@ -23,19 +23,25 @@ PAIR = 2
 PAIR_COLS = PAIR * K_PASS
 N_PAIRS = sum(WIDTHS) // PAIR_COLS
 UNIT = 4
-LATE_PAIRS = UNIT
+LATE_PAIRS = 2
 FIRST_LATE = N_PAIRS - LATE_PAIRS
-KEYS_EVERY = 3
-AHEAD = 3
-RAW_BUFS = 2 * (AHEAD + 1)
-EMPTY_BOTH = "SVSVSSVS"
-EMPTY_KEYS = "SVSV"
-EMPTY_LATE = "SSVS"
+KEYS_EVERY = 6
+RAW_BUFS = 8
+AHEAD = RAW_BUFS - 2
+RUN_BANKS = 3
+MIN_MATMULS = 2
+FIRST_FILLERS = 6
+LAG_BANKS = 4
+TAIL_PASSES = 4
+EMPTY = "SVSS"
 SCORE_SCALE = 1.0 / 32.0
 HALVES = 2
 VALUE_PARTS = 4
 VALUE_COLS = E // VALUE_PARTS
-VALUE_STEP = 6
+VALUE_UNIT = 18
+VALUE_SLOT = 22
+BIFURCATE_SLOT = 10
+SLOTS_BETWEEN = 2
 
 FLOPS = 2 * S * S * (E + 2 * HALF) + 2 * S * S * E
 
@@ -66,17 +72,21 @@ def tile_chaoticattentionmechanism_pb_k_kernel(
             for col in range(0, width, PAIR_COLS):
                 pairs.append((array_index, col))
 
-        steps = []
+        units = []
         late = FIRST_LATE
         for pair in range(FIRST_LATE):
-            steps.append((pair, [(m, pair) for m in range(TILES)]))
-            if pair % KEYS_EVERY == KEYS_EVERY - 1 and late < N_PAIRS:
-                steps.append((late, []))
+            units.append(("key", pair))
+            units.append(("query", [(m, pair) for m in range(TILES)]))
+            if pair % KEYS_EVERY == KEYS_EVERY - 1:
+                units.append(("key", late))
                 late += 1
-        for m in range(TILES):
-            steps.append((None, [(m, pair) for pair in range(FIRST_LATE, N_PAIRS)]))
+        for m in range(0, TILES, UNIT // LATE_PAIRS):
+            units.append(
+                ("query", [(m + j // LATE_PAIRS, FIRST_LATE + j % LATE_PAIRS) for j in range(UNIT)])
+            )
 
         raw = {}
+        grouped = {}
         key_codes = {}
         key_scales = {}
         query_codes = {}
@@ -95,100 +105,87 @@ def tile_chaoticattentionmechanism_pb_k_kernel(
         def new_raw():
             return raw_pool.tile([P, UNIT, PAIR_COLS], BF16, tag="raw", name="loaded")
 
-        def load_step(i, pieces):
-            key_pair, queries = steps[i]
-            if key_pair is not None:
-                array_index, col = pairs[key_pair]
-                raw[(i, "key")] = new_raw()
-                for c in range(0, UNIT, UNIT // pieces):
-                    nc.sync.dma_start(
-                        out=raw[(i, "key")][:, c : c + UNIT // pieces, :],
-                        in_=key_rows[array_index][:, c : c + UNIT // pieces, col : col + PAIR_COLS],
-                    )
-            if queries:
-                m, pair = queries[0]
+        def load_unit(n, pieces):
+            side, what = units[n]
+            raw[n] = new_raw()
+            target = raw[n][:]
+            if side == "key":
+                array_index, col = pairs[what]
+                source = key_rows[array_index][:, :, col : col + PAIR_COLS]
+            else:
+                m, pair = what[0]
                 array_index, col = pairs[pair]
-                raw[(i, "query")] = new_raw()
-                if key_pair is not None:
+                if pair < FIRST_LATE:
                     source = query_rows[array_index][:, :, col : col + PAIR_COLS]
                 else:
-                    source = query_rows[array_index][:, m, col : col + UNIT * PAIR_COLS].rearrange(
-                        "p (j k) -> p j k", j=UNIT
-                    )
-                for c in range(0, UNIT, UNIT // pieces):
-                    nc.sync.dma_start(
-                        out=raw[(i, "query")][:, c : c + UNIT // pieces, :], in_=source[:, c : c + UNIT // pieces, :]
-                    )
-
-        def transpose_unit(loaded, views, engines):
-            words = loaded[:].bitcast(F32)
-            for c in range(UNIT):
-                bank = psum_work.tile([P, PAIR, 2, P], F32, tag="work", name="bank")
-                for s in range(PAIR):
-                    for u in range(2):
-                        w0 = (2 * s + u) * P
-                        nc.tensor.transpose(bank[:, s, u, :], words[:, c, w0 : w0 + P], ident_f32[:])
-                if engines[c] == "S":
-                    nc.scalar.copy(out=views[c], in_=bank[:].rearrange("p s u r -> p s r u"))
-                else:
-                    nc.vector.tensor_copy(out=views[c], in_=bank[:].rearrange("p s u r -> p s r u"))
-
-        def transpose_step(i):
-            key_pair, queries = steps[i]
-            grouped_keys = None
-            grouped_queries = None
-            if key_pair is not None:
-                grouped_keys = stage.tile([P, PAIR * S * PACK], BF16, tag="grouped_keys", align_bytes=64)
-                words = grouped_keys[:].bitcast(F32).rearrange("p (s t r u) -> p s t r u", s=PAIR, t=TILES, u=2)
-                engines = EMPTY_BOTH if queries else EMPTY_KEYS
-                transpose_unit(raw[(i, "key")], [words[:, :, t] for t in range(TILES)], engines)
-            if queries:
-                grouped_queries = stage.tile([P, UNIT * PAIR * P * PACK], BF16, tag="grouped_queries", align_bytes=64)
-                words = grouped_queries[:].bitcast(F32).rearrange("p (j s r u) -> p j s r u", j=UNIT, s=PAIR, u=2)
-                engines = EMPTY_LATE if key_pair is None else EMPTY_BOTH[UNIT:]
-                transpose_unit(raw[(i, "query")], [words[:, j] for j in range(UNIT)], engines)
-            if key_pair is not None:
-                key_codes[key_pair] = keep.tile(
-                    [P, PAIR * S], U32, name="key_codes_%d" % key_pair, align_bytes=64
-                )
-                key_scales[key_pair] = keep.tile(
-                    [P, PAIR * S], U8, name="key_scales_%d" % key_pair, align_bytes=64
-                )
-                nc.vector.quantize_mx(
-                    out=key_codes[key_pair][:].bitcast(FP8X4), scales=key_scales[key_pair][:], in_=grouped_keys[:]
-                )
-            if queries:
-                n_words = UNIT * PAIR * P
-                query_codes[i] = stage.tile([P, n_words], U32, tag="query_codes", name="codes", align_bytes=64)
-                query_scales[i] = stage.tile([P, n_words], U8, tag="query_scales", name="scales", align_bytes=64)
-                nc.vector.quantize_mx(
-                    out=query_codes[i][:].bitcast(FP8X4), scales=query_scales[i][:], in_=grouped_queries[:]
+                    source = query_rows[array_index][:, m : m + UNIT // LATE_PAIRS, col : col + LATE_PAIRS * PAIR_COLS]
+                    target = target.rearrange("p (m j) k -> p m (j k)", j=LATE_PAIRS)
+            step = target.shape[1] // pieces
+            for c in range(pieces):
+                nc.sync.dma_start(
+                    out=target[:, c * step : (c + 1) * step, :], in_=source[:, c * step : (c + 1) * step, :]
                 )
 
-        def multiply_step(i):
-            closed = []
-            for j, (m, pair) in enumerate(steps[i][1]):
-                for s in range(PAIR):
-                    opens = pair <= 1 and s == 0
-                    closes = pair in (0, N_PAIRS - 1) and s == PAIR - 1
-                    if opens and pair == 0:
-                        score_bank[m] = psum_sync.tile([P, S], F32, tag="sums", name="score_bank")
-                    if opens and pair == 1:
-                        sync_bank[m] = psum_sync.tile([P, S], F32, tag="sums", name="sync_bank")
-                    query_cols = slice((j * PAIR + s) * P, (j * PAIR + s + 1) * P)
-                    key_cols = slice(s * S, (s + 1) * S)
-                    nc.tensor.matmul_mx(
-                        out=(score_bank if pair == 0 else sync_bank)[m][:],
-                        lhsT=query_codes[i][:, query_cols].bitcast(FP8X4),
-                        lhsT_scale=query_scales[i][:, query_cols],
-                        rhs=key_codes[pair][:, key_cols].bitcast(FP8X4),
-                        rhs_scale=key_scales[pair][:, key_cols],
-                        start=opens,
-                        stop=closes,
-                    )
-                    if closes and pair > 0:
-                        closed.append(m)
-            return closed
+        def transpose_bank(n, c, fillers):
+            if c == 0:
+                grouped[n] = stage.tile(
+                    [P, UNIT * PAIR * P * PACK], BF16, tag="grouped_%s" % units[n][0], name="grouped", align_bytes=64
+                )
+            values = grouped[n][:].bitcast(F32)
+            if units[n][0] == "key":
+                view = values.rearrange("p (s t r u) -> p s t r u", s=PAIR, t=TILES, u=2)[:, :, c]
+            else:
+                view = values.rearrange("p (j s r u) -> p j s r u", j=UNIT, s=PAIR, u=2)[:, c]
+            words = raw[n][:].bitcast(F32)
+            bank = psum_work.tile([P, PAIR, 2, P], F32, tag="work", name="bank")
+            for f in range(fillers):
+                nc.tensor.matmul(
+                    bank[:].rearrange("p s u r -> p (s u r)"), lhsT=zeros[:, 0:P], rhs=zeros[:], start=True, stop=True
+                )
+            for s in range(PAIR):
+                for u in range(2):
+                    w0 = (2 * s + u) * P
+                    nc.tensor.transpose(bank[:, s, u, :], words[:, c, w0 : w0 + P], ident_f32[:])
+            if EMPTY[c] == "S":
+                nc.scalar.copy(out=view, in_=bank[:].rearrange("p s u r -> p s r u"))
+            else:
+                nc.vector.tensor_copy(out=view, in_=bank[:].rearrange("p s u r -> p s r u"))
+
+        def quantise_unit(n):
+            side, what = units[n]
+            n_words = UNIT * PAIR * P
+            if side == "key":
+                codes = keep.tile([P, n_words], U32, name="key_codes_%d" % what, align_bytes=64)
+                scales = keep.tile([P, n_words], U8, name="key_scales_%d" % what, align_bytes=64)
+                key_codes[what] = codes
+                key_scales[what] = scales
+            else:
+                codes = stage.tile([P, n_words], U32, tag="query_codes", name="codes", align_bytes=64)
+                scales = stage.tile([P, n_words], U8, tag="query_scales", name="scales", align_bytes=64)
+                query_codes[n] = codes
+                query_scales[n] = scales
+            nc.vector.quantize_mx(out=codes[:].bitcast(FP8X4), scales=scales[:], in_=grouped[n][:])
+
+        def multiply(n, j, s):
+            m, pair = units[n][1][j]
+            opens = pair <= 1 and s == 0
+            closes = pair in (0, N_PAIRS - 1) and s == PAIR - 1
+            if opens and pair == 0:
+                score_bank[m] = psum_sync.tile([P, S], F32, tag="sums", name="score_bank")
+            if opens and pair == 1:
+                sync_bank[m] = psum_sync.tile([P, S], F32, tag="sums", name="sync_bank")
+            query_cols = slice((j * PAIR + s) * P, (j * PAIR + s + 1) * P)
+            key_cols = slice(s * S, (s + 1) * S)
+            nc.tensor.matmul_mx(
+                out=(score_bank if pair == 0 else sync_bank)[m][:],
+                lhsT=query_codes[n][:, query_cols].bitcast(FP8X4),
+                lhsT_scale=query_scales[n][:, query_cols],
+                rhs=key_codes[pair][:, key_cols].bitcast(FP8X4),
+                rhs_scale=key_scales[pair][:, key_cols],
+                start=opens,
+                stop=closes,
+            )
+            return (m, pair) if closes else None
 
         def empty_scores(m):
             tanh[m] = keep.tile([P, S], F32, name="tanh_%d" % m)
@@ -272,13 +269,16 @@ def tile_chaoticattentionmechanism_pb_k_kernel(
                     )
                 nc.sync.dma_start(out=out_rows[m][:, h * S : (h + 1) * S], in_=result[:, h * S : (h + 1) * S])
 
-        load_step(0, UNIT)
-        for i in range(1, AHEAD):
-            load_step(i, 2)
+        load_unit(0, UNIT)
+        load_unit(1, UNIT)
+        for n in range(2, AHEAD):
+            load_unit(n, 2)
         bif_raw = keep.tile([P, 1], BF16)
         nc.scalar.dma_start(out=bif_raw[:], in_=bifurcation_param.partition_broadcast(P))
         coupling_raw = keep.tile([P, 1], BF16)
         nc.scalar.dma_start(out=coupling_raw[:], in_=phase_coupling.partition_broadcast(P))
+        zeros = keep.tile([P, S], BF16)
+        nc.vector.memset(zeros[:], 0.0)
         ident_f32 = keep.tile([P, P], F32)
         make_identity(nc, ident_f32[:])
         ident_bf16 = keep.tile([P, P], BF16)
@@ -293,35 +293,65 @@ def tile_chaoticattentionmechanism_pb_k_kernel(
         value_codes = keep.tile([P, E], U32, align_bytes=64)
         value_scales = keep.tile([P, E], U8, align_bytes=64)
 
-        to_transpose = []
-        to_weigh = []
-        for i in range(len(steps) + 3):
-            if i + AHEAD < len(steps):
-                load_step(i + AHEAD, 2)
-            if i == VALUE_STEP - AHEAD:
-                raw["values"] = new_raw()
-                nc.sync.dma_start(out=raw["values"][:], in_=value_rows)
-            if i < len(steps):
-                transpose_step(i)
-            for m in to_weigh:
-                quantise_weights(m)
-                weigh_values(m)
-            closed = []
-            if 1 <= i <= len(steps):
-                closed = multiply_step(i - 1)
-            if i == 1:
-                for m in range(TILES):
-                    empty_scores(m)
-            if 2 <= i < 2 + TILES:
-                bifurcate(i - 2)
-            for m in closed:
-                softmax_rows(m)
-            for m in to_transpose:
-                transpose_weights(m)
+        banks = [(n, c) for n in range(len(units)) for c in range(UNIT)]
+        queue = []
+        done = 0
+        fillers = FIRST_FILLERS
+        sent = 0
+        after = {}
+        last_slot = 0
+        slot = 0
+        while done < len(banks) or sent < len(queue) or slot <= last_slot:
+            for n, c in banks[done : done + RUN_BANKS]:
+                if c == 0 and n + AHEAD < len(units):
+                    load_unit(n + AHEAD, 2)
+                if c == 0 and n + AHEAD == VALUE_UNIT:
+                    raw["values"] = new_raw()
+                    nc.sync.dma_start(out=raw["values"][:], in_=value_rows)
+                transpose_bank(n, c, fillers)
+                fillers = 0
+                done += 1
+                quantised = None
+                if c == 1 and n > 0:
+                    quantised = n - 1
+                elif done == len(banks):
+                    quantised = n
+                if quantised is not None:
+                    quantise_unit(quantised)
+                    if units[quantised][0] == "query":
+                        for j in range(UNIT):
+                            for s in range(PAIR):
+                                queue.append((done + LAG_BANKS, (quantised, j, s)))
+            tail = done == len(banks)
+            tasks = after.get(slot, [])
+            for what, m in tasks:
+                if what == "weigh":
+                    quantise_weights(m)
+                    weigh_values(m)
+            count = 0
+            while (
+                sent < len(queue) and count < (TAIL_PASSES if tail else RUN_BANKS) and (tail or queue[sent][0] <= done)
+            ):
+                closed = multiply(*queue[sent][1])
+                sent += 1
+                count += 1
+                if closed is not None and closed[1] == 0:
+                    empty_scores(closed[0])
+                elif closed is not None:
+                    softmax_rows(closed[0])
+                    after.setdefault(slot + 2, []).append(("transpose", closed[0]))
+                    after.setdefault(slot + 3, []).append(("weigh", closed[0]))
+                    last_slot = slot + 3
+            fillers = max(0, MIN_MATMULS - count)
+            for what, m in tasks:
+                if what == "transpose":
+                    transpose_weights(m)
+            for m in range(TILES):
+                if slot == BIFURCATE_SLOT + SLOTS_BETWEEN * m:
+                    bifurcate(m)
             for part in range(VALUE_PARTS):
-                if i == VALUE_STEP + part:
+                if slot == VALUE_SLOT + SLOTS_BETWEEN * part:
                     regroup_values(part)
-                if i == VALUE_STEP + part + 1:
+                if slot == VALUE_SLOT + SLOTS_BETWEEN * part + 1:
                     quantise_values(part)
-            to_weigh = to_transpose
-            to_transpose = closed
+            slot += 1

@@ -23,25 +23,21 @@ PAIR = 2
 PAIR_COLS = PAIR * K_PASS
 N_PAIRS = sum(WIDTHS) // PAIR_COLS
 UNIT = 4
-LATE_PAIRS = 2
+LATE_PAIRS = UNIT
 FIRST_LATE = N_PAIRS - LATE_PAIRS
-KEYS_EVERY = 6
+KEYS_EVERY = 3
 RAW_BUFS = 8
 AHEAD = RAW_BUFS - 2
-RUN_BANKS = 3
-MIN_MATMULS = 2
-FIRST_FILLERS = 6
-LAG_BANKS = 4
-TAIL_PASSES = 4
+FIRST_FILLERS = 4
+HEAD_FILLERS = 2
 EMPTY = "SVSS"
+PARTS = 2
 SCORE_SCALE = 1.0 / 32.0
 HALVES = 2
 VALUE_PARTS = 4
 VALUE_COLS = E // VALUE_PARTS
 VALUE_UNIT = 18
-VALUE_SLOT = 22
-BIFURCATE_SLOT = 10
-SLOTS_BETWEEN = 2
+BIFURCATE_UNIT = 6
 
 FLOPS = 2 * S * S * (E + 2 * HALF) + 2 * S * S * E
 
@@ -80,10 +76,9 @@ def tile_chaoticattentionmechanism_pb_k_kernel(
             if pair % KEYS_EVERY == KEYS_EVERY - 1:
                 units.append(("key", late))
                 late += 1
-        for m in range(0, TILES, UNIT // LATE_PAIRS):
-            units.append(
-                ("query", [(m + j // LATE_PAIRS, FIRST_LATE + j % LATE_PAIRS) for j in range(UNIT)])
-            )
+        n_main = len(units)
+        for m in range(TILES):
+            units.append(("query", [(m, pair) for pair in range(FIRST_LATE, N_PAIRS)]))
 
         raw = {}
         grouped = {}
@@ -108,7 +103,6 @@ def tile_chaoticattentionmechanism_pb_k_kernel(
         def load_unit(n, pieces):
             side, what = units[n]
             raw[n] = new_raw()
-            target = raw[n][:]
             if side == "key":
                 array_index, col = pairs[what]
                 source = key_rows[array_index][:, :, col : col + PAIR_COLS]
@@ -118,13 +112,12 @@ def tile_chaoticattentionmechanism_pb_k_kernel(
                 if pair < FIRST_LATE:
                     source = query_rows[array_index][:, :, col : col + PAIR_COLS]
                 else:
-                    source = query_rows[array_index][:, m : m + UNIT // LATE_PAIRS, col : col + LATE_PAIRS * PAIR_COLS]
-                    target = target.rearrange("p (m j) k -> p m (j k)", j=LATE_PAIRS)
-            step = target.shape[1] // pieces
-            for c in range(pieces):
-                nc.sync.dma_start(
-                    out=target[:, c * step : (c + 1) * step, :], in_=source[:, c * step : (c + 1) * step, :]
-                )
+                    source = query_rows[array_index][:, m, col : col + UNIT * PAIR_COLS].rearrange(
+                        "p (j k) -> p j k", j=UNIT
+                    )
+            step = UNIT // pieces
+            for c in range(0, UNIT, step):
+                nc.sync.dma_start(out=raw[n][:, c : c + step, :], in_=source[:, c : c + step, :])
 
         def transpose_bank(n, c, fillers):
             if c == 0:
@@ -151,20 +144,25 @@ def tile_chaoticattentionmechanism_pb_k_kernel(
             else:
                 nc.vector.tensor_copy(out=view, in_=bank[:].rearrange("p s u r -> p s r u"))
 
-        def quantise_unit(n):
-            side, what = units[n]
+        def quantise_keys(n):
+            pair = units[n][1]
+            key_codes[pair] = keep.tile([P, PAIR * S], U32, name="key_codes_%d" % pair, align_bytes=64)
+            key_scales[pair] = keep.tile([P, PAIR * S], U8, name="key_scales_%d" % pair, align_bytes=64)
+            nc.vector.quantize_mx(
+                out=key_codes[pair][:].bitcast(FP8X4), scales=key_scales[pair][:], in_=grouped[n][:]
+            )
+
+        def quantise_queries(n, part):
             n_words = UNIT * PAIR * P
-            if side == "key":
-                codes = keep.tile([P, n_words], U32, name="key_codes_%d" % what, align_bytes=64)
-                scales = keep.tile([P, n_words], U8, name="key_scales_%d" % what, align_bytes=64)
-                key_codes[what] = codes
-                key_scales[what] = scales
-            else:
-                codes = stage.tile([P, n_words], U32, tag="query_codes", name="codes", align_bytes=64)
-                scales = stage.tile([P, n_words], U8, tag="query_scales", name="scales", align_bytes=64)
-                query_codes[n] = codes
-                query_scales[n] = scales
-            nc.vector.quantize_mx(out=codes[:].bitcast(FP8X4), scales=scales[:], in_=grouped[n][:])
+            if part == 0:
+                query_codes[n] = stage.tile([P, n_words], U32, tag="query_codes", name="codes", bufs=3, align_bytes=64)
+                query_scales[n] = stage.tile([P, n_words], U8, tag="query_scales", name="scales", bufs=3, align_bytes=64)
+            words = slice(part * n_words // PARTS, (part + 1) * n_words // PARTS)
+            nc.vector.quantize_mx(
+                out=query_codes[n][:, words].bitcast(FP8X4),
+                scales=query_scales[n][:, words],
+                in_=grouped[n][:, words.start * PACK : words.stop * PACK],
+            )
 
         def multiply(n, j, s):
             m, pair = units[n][1][j]
@@ -188,7 +186,7 @@ def tile_chaoticattentionmechanism_pb_k_kernel(
             return (m, pair) if closes else None
 
         def empty_scores(m):
-            tanh[m] = keep.tile([P, S], F32, name="tanh_%d" % m)
+            tanh[m] = stage.tile([P, S], F32, tag="tanh", name="tanh", bufs=TILES)
             nc.scalar.activation(out=tanh[m][:], in_=score_bank[m][:], func=ACT.Tanh, scale=SCORE_SCALE)
             base[m] = keep.tile([P, S], F32, name="base_%d" % m)
             nc.vector.tensor_scalar(
@@ -246,28 +244,29 @@ def tile_chaoticattentionmechanism_pb_k_kernel(
                 in_=grouped_values[part][:].rearrange("p w j -> p (w j)"),
             )
 
-        def weigh_values(m):
+        def weigh_values(m, engines):
             inv_sum = stage.tile([P, 1], F32, tag="inv_sum")
             nc.vector.reciprocal(inv_sum[:], row_sum[m][:])
             result = stage.tile([P, HALVES * S], F32, tag="result")
             for h in range(HALVES):
+                cols = slice(h * S, (h + 1) * S)
                 product = psum_work.tile([P, S], F32, tag="work", name="product")
                 nc.tensor.matmul_mx(
                     out=product[:],
                     lhsT=weight_codes[m][:].bitcast(FP8X4),
                     lhsT_scale=weight_scales[m][:],
-                    rhs=value_codes[:, h * S : (h + 1) * S].bitcast(FP8X4),
-                    rhs_scale=value_scales[:, h * S : (h + 1) * S],
+                    rhs=value_codes[:, cols].bitcast(FP8X4),
+                    rhs_scale=value_scales[:, cols],
                     start=True,
                     stop=True,
                 )
-                if h == 0:
-                    nc.scalar.activation(out=result[:, 0:S], in_=product[:], func=ACT.Copy, scale=inv_sum[:, 0:1])
+                if engines[h] == "S":
+                    nc.scalar.activation(out=result[:, cols], in_=product[:], func=ACT.Copy, scale=inv_sum[:, 0:1])
                 else:
                     nc.vector.tensor_scalar(
-                        out=result[:, S : 2 * S], in0=product[:], scalar1=inv_sum[:, 0:1], scalar2=None, op0=ALU.mult
+                        out=result[:, cols], in0=product[:], scalar1=inv_sum[:, 0:1], scalar2=None, op0=ALU.mult
                     )
-                nc.sync.dma_start(out=out_rows[m][:, h * S : (h + 1) * S], in_=result[:, h * S : (h + 1) * S])
+                nc.sync.dma_start(out=out_rows[m][:, cols], in_=result[:, cols])
 
         load_unit(0, UNIT)
         load_unit(1, UNIT)
@@ -293,65 +292,65 @@ def tile_chaoticattentionmechanism_pb_k_kernel(
         value_codes = keep.tile([P, E], U32, align_bytes=64)
         value_scales = keep.tile([P, E], U8, align_bytes=64)
 
-        banks = [(n, c) for n in range(len(units)) for c in range(UNIT)]
         queue = []
-        done = 0
-        fillers = FIRST_FILLERS
         sent = 0
-        after = {}
-        last_slot = 0
-        slot = 0
-        while done < len(banks) or sent < len(queue) or slot <= last_slot:
-            for n, c in banks[done : done + RUN_BANKS]:
+        n_passes = FIRST_LATE * UNIT * PAIR
+
+        def transpose_unit(n, fillers):
+            for c in range(UNIT):
                 if c == 0 and n + AHEAD < len(units):
                     load_unit(n + AHEAD, 2)
-                if c == 0 and n + AHEAD == VALUE_UNIT:
-                    raw["values"] = new_raw()
-                    nc.sync.dma_start(out=raw["values"][:], in_=value_rows)
-                transpose_bank(n, c, fillers)
-                fillers = 0
-                done += 1
-                quantised = None
-                if c == 1 and n > 0:
-                    quantised = n - 1
-                elif done == len(banks):
-                    quantised = n
-                if quantised is not None:
-                    quantise_unit(quantised)
-                    if units[quantised][0] == "query":
-                        for j in range(UNIT):
-                            for s in range(PAIR):
-                                queue.append((done + LAG_BANKS, (quantised, j, s)))
-            tail = done == len(banks)
-            tasks = after.get(slot, [])
-            for what, m in tasks:
-                if what == "weigh":
-                    quantise_weights(m)
-                    weigh_values(m)
-            count = 0
-            while (
-                sent < len(queue) and count < (TAIL_PASSES if tail else RUN_BANKS) and (tail or queue[sent][0] <= done)
-            ):
-                closed = multiply(*queue[sent][1])
+                transpose_bank(n, c, fillers if c == 0 else 0)
+                if c == 0 and n > 0:
+                    if units[n - 1][0] == "key":
+                        quantise_keys(n - 1)
+                    else:
+                        quantise_queries(n - 1, 1)
+                if c == 2 and units[n][0] == "query":
+                    quantise_queries(n, 0)
+
+        for n in range(n_main):
+            transpose_unit(n, FIRST_FILLERS if n == 0 else HEAD_FILLERS if sent == 0 else 0)
+            if n + AHEAD == VALUE_UNIT:
+                raw["values"] = new_raw()
+                nc.sync.dma_start(out=raw["values"][:], in_=value_rows)
+            if n > 0 and units[n - 1][0] == "query":
+                for j in range(UNIT):
+                    for s in range(PAIR):
+                        queue.append((n - 1, j, s))
+            while sent < len(queue) and sent < (n - 1) * n_passes // n_main:
+                closed = multiply(*queue[sent])
                 sent += 1
-                count += 1
-                if closed is not None and closed[1] == 0:
+                if closed is not None:
                     empty_scores(closed[0])
-                elif closed is not None:
-                    softmax_rows(closed[0])
-                    after.setdefault(slot + 2, []).append(("transpose", closed[0]))
-                    after.setdefault(slot + 3, []).append(("weigh", closed[0]))
-                    last_slot = slot + 3
-            fillers = max(0, MIN_MATMULS - count)
-            for what, m in tasks:
-                if what == "transpose":
-                    transpose_weights(m)
-            for m in range(TILES):
-                if slot == BIFURCATE_SLOT + SLOTS_BETWEEN * m:
-                    bifurcate(m)
-            for part in range(VALUE_PARTS):
-                if slot == VALUE_SLOT + SLOTS_BETWEEN * part:
-                    regroup_values(part)
-                if slot == VALUE_SLOT + SLOTS_BETWEEN * part + 1:
-                    quantise_values(part)
-            slot += 1
+            if BIFURCATE_UNIT <= n < BIFURCATE_UNIT + TILES:
+                bifurcate(n - BIFURCATE_UNIT)
+            if VALUE_UNIT <= n < VALUE_UNIT + VALUE_PARTS:
+                regroup_values(n - VALUE_UNIT)
+            if VALUE_UNIT < n <= VALUE_UNIT + VALUE_PARTS:
+                quantise_values(n - VALUE_UNIT - 1)
+
+        for m in range(TILES + 1):
+            if m < TILES:
+                transpose_unit(n_main + m, 0)
+            else:
+                quantise_queries(n_main + m - 1, 1)
+            if m == 0:
+                queue.extend([(n_main - 1, j, s) for j in range(UNIT) for s in range(PAIR)])
+                for item in queue[sent:]:
+                    multiply(*item)
+                continue
+            passes = [(n_main + m - 1, j, s) for j in range(UNIT) for s in range(PAIR)]
+            for index, item in enumerate(passes):
+                if index == len(passes) // 2 and m >= 3:
+                    quantise_weights(m - 3)
+                    weigh_values(m - 3, "SV")
+                multiply(*item)
+            if m >= 2:
+                transpose_weights(m - 2)
+            softmax_rows(m - 1)
+        quantise_weights(TILES - 2)
+        weigh_values(TILES - 2, "VV")
+        transpose_weights(TILES - 1)
+        quantise_weights(TILES - 1)
+        weigh_values(TILES - 1, "SV")

@@ -32,6 +32,8 @@ FIRST_FILLERS = 4
 HEAD_FILLERS = 2
 EMPTY = "SVSS"
 PARTS = 2
+RUN = 3
+LATE_RUN = 2
 SCORE_SCALE = 1.0 / 32.0
 HALVES = 2
 VALUE_PARTS = 4
@@ -295,34 +297,39 @@ def tile_chaoticattentionmechanism_pb_k_kernel(
         queue = []
         sent = 0
         n_passes = FIRST_LATE * UNIT * PAIR
+        n_banks = n_main * UNIT
+        first_pass_bank = 2 * UNIT
 
-        def transpose_unit(n, fillers):
-            for c in range(UNIT):
-                if c == 0 and n + AHEAD < len(units):
-                    load_unit(n + AHEAD, 2)
-                transpose_bank(n, c, fillers if c == 0 else 0)
-                if c == 0 and n > 0:
-                    if units[n - 1][0] == "key":
-                        quantise_keys(n - 1)
-                    else:
-                        quantise_queries(n - 1, 1)
-                if c == 2 and units[n][0] == "query":
-                    quantise_queries(n, 0)
+        def passes_of(n):
+            return [(n, j, s) for j in range(UNIT) for s in range(PAIR)]
+
+        def transpose_piece(n, c, fillers):
+            if c == 0 and n + AHEAD < len(units):
+                load_unit(n + AHEAD, 2)
+            transpose_bank(n, c, fillers)
+            if c == 0 and n > 0:
+                if units[n - 1][0] == "key":
+                    quantise_keys(n - 1)
+                else:
+                    quantise_queries(n - 1, 1)
+            if c == 2 and units[n][0] == "query":
+                quantise_queries(n, 0)
 
         for n in range(n_main):
-            transpose_unit(n, FIRST_FILLERS if n == 0 else HEAD_FILLERS if sent == 0 else 0)
+            for c in range(UNIT):
+                done = n * UNIT + c + 1
+                transpose_piece(n, c, 0 if c > 0 or sent > 0 else FIRST_FILLERS if n == 0 else HEAD_FILLERS)
+                if c == 0 and n > 0 and units[n - 1][0] == "query":
+                    queue.extend(passes_of(n - 1))
+                if done % RUN == 0:
+                    while sent < len(queue) and sent < (done - first_pass_bank) * n_passes // n_banks:
+                        closed = multiply(*queue[sent])
+                        sent += 1
+                        if closed is not None:
+                            empty_scores(closed[0])
             if n + AHEAD == VALUE_UNIT:
                 raw["values"] = new_raw()
                 nc.sync.dma_start(out=raw["values"][:], in_=value_rows)
-            if n > 0 and units[n - 1][0] == "query":
-                for j in range(UNIT):
-                    for s in range(PAIR):
-                        queue.append((n - 1, j, s))
-            while sent < len(queue) and sent < (n - 1) * n_passes // n_main:
-                closed = multiply(*queue[sent])
-                sent += 1
-                if closed is not None:
-                    empty_scores(closed[0])
             if BIFURCATE_UNIT <= n < BIFURCATE_UNIT + TILES:
                 bifurcate(n - BIFURCATE_UNIT)
             if VALUE_UNIT <= n < VALUE_UNIT + VALUE_PARTS:
@@ -330,22 +337,23 @@ def tile_chaoticattentionmechanism_pb_k_kernel(
             if VALUE_UNIT < n <= VALUE_UNIT + VALUE_PARTS:
                 quantise_values(n - VALUE_UNIT - 1)
 
+        queue.extend(passes_of(n_main - 1))
         for m in range(TILES + 1):
-            if m < TILES:
-                transpose_unit(n_main + m, 0)
-            else:
-                quantise_queries(n_main + m - 1, 1)
-            if m == 0:
-                queue.extend([(n_main - 1, j, s) for j in range(UNIT) for s in range(PAIR)])
-                for item in queue[sent:]:
-                    multiply(*item)
-                continue
-            passes = [(n_main + m - 1, j, s) for j in range(UNIT) for s in range(PAIR)]
-            for index, item in enumerate(passes):
-                if index == len(passes) // 2 and m >= 3:
+            passes = queue[sent:] if m == 0 else passes_of(n_main + m - 1)
+            runs = UNIT // LATE_RUN
+            for run in range(runs):
+                if m < TILES:
+                    for c in range(run * LATE_RUN, (run + 1) * LATE_RUN):
+                        transpose_piece(n_main + m, c, 0)
+                elif run == 0:
+                    quantise_queries(n_main + m - 1, 1)
+                if run == runs - 1 and m >= 3:
                     quantise_weights(m - 3)
                     weigh_values(m - 3, "SV")
-                multiply(*item)
+                for item in passes[run * len(passes) // runs : (run + 1) * len(passes) // runs]:
+                    multiply(*item)
+            if m == 0:
+                continue
             if m >= 2:
                 transpose_weights(m - 2)
             softmax_rows(m - 1)

@@ -32,8 +32,8 @@ FIRST_FILLERS = 4
 HEAD_FILLERS = 2
 EMPTY = "SVSS"
 PARTS = 2
-RUN = 3
-LATE_RUN = 2
+RUN = 6
+LATE_RUN = 4
 SCORE_SCALE = 1.0 / 32.0
 HALVES = 2
 VALUE_PARTS = 4

@@ -25,15 +25,14 @@ N_PAIRS = sum(WIDTHS) // PAIR_COLS
 UNIT = 4
 LATE_PAIRS = UNIT
 FIRST_LATE = N_PAIRS - LATE_PAIRS
-KEYS_EVERY = 3
+KEYS_FROM = FIRST_LATE - LATE_PAIRS
 RAW_BUFS = 8
 AHEAD = RAW_BUFS - 2
 FIRST_FILLERS = 4
 HEAD_FILLERS = 2
-EMPTY = "SVSS"
+EMPTY = "VSSS"
 PARTS = 2
-RUN = 6
-LATE_RUN = 4
+RUN = 4
 SCORE_SCALE = 1.0 / 32.0
 HALVES = 2
 VALUE_PARTS = 4
@@ -65,17 +64,19 @@ def tile_chaoticattentionmechanism_pb_k_kernel(
         value_rows = V.rearrange("b s w -> (b s) w").rearrange("(p j) w -> p j w", j=PACK)
         out_rows = out.rearrange("b s w -> (b s) w").rearrange("(m p) w -> m p w", p=P)
 
-        pairs = []
-        for array_index, width in enumerate(WIDTHS):
-            for col in range(0, width, PAIR_COLS):
-                pairs.append((array_index, col))
+        pairs = [(0, 0)]
+        for array_index, n_far in ((1, 8), (2, 4)):
+            for i in range(n_far // 2):
+                for half in range(2):
+                    pairs.append((array_index, (i + half * n_far // 2) * PAIR_COLS))
+        pairs.extend([(2, (4 + i) * PAIR_COLS) for i in range(LATE_PAIRS)])
 
         units = []
         late = FIRST_LATE
         for pair in range(FIRST_LATE):
             units.append(("key", pair))
             units.append(("query", [(m, pair) for m in range(TILES)]))
-            if pair % KEYS_EVERY == KEYS_EVERY - 1:
+            if pair >= KEYS_FROM:
                 units.append(("key", late))
                 late += 1
         n_main = len(units)
@@ -148,8 +149,8 @@ def tile_chaoticattentionmechanism_pb_k_kernel(
 
         def quantise_keys(n):
             pair = units[n][1]
-            key_codes[pair] = keep.tile([P, PAIR * S], U32, name="key_codes_%d" % pair, align_bytes=64)
-            key_scales[pair] = keep.tile([P, PAIR * S], U8, name="key_scales_%d" % pair, align_bytes=64)
+            key_codes[pair] = keep.tile([P, PAIR * S], U32, name="key_codes_%d" % pair, align_bytes=256)
+            key_scales[pair] = keep.tile([P, PAIR * S], U8, name="key_scales_%d" % pair, align_bytes=256)
             nc.vector.quantize_mx(
                 out=key_codes[pair][:].bitcast(FP8X4), scales=key_scales[pair][:], in_=grouped[n][:]
             )
@@ -157,8 +158,8 @@ def tile_chaoticattentionmechanism_pb_k_kernel(
         def quantise_queries(n, part):
             n_words = UNIT * PAIR * P
             if part == 0:
-                query_codes[n] = stage.tile([P, n_words], U32, tag="query_codes", name="codes", bufs=3, align_bytes=64)
-                query_scales[n] = stage.tile([P, n_words], U8, tag="query_scales", name="scales", bufs=3, align_bytes=64)
+                query_codes[n] = stage.tile([P, n_words], U32, tag="query_codes", name="codes", bufs=3, align_bytes=256)
+                query_scales[n] = stage.tile([P, n_words], U8, tag="query_scales", name="scales", bufs=3, align_bytes=256)
             words = slice(part * n_words // PARTS, (part + 1) * n_words // PARTS)
             nc.vector.quantize_mx(
                 out=query_codes[n][:, words].bitcast(FP8X4),
@@ -188,8 +189,10 @@ def tile_chaoticattentionmechanism_pb_k_kernel(
             return (m, pair) if closes else None
 
         def empty_scores(m):
-            tanh[m] = stage.tile([P, S], F32, tag="tanh", name="tanh", bufs=TILES)
-            nc.scalar.activation(out=tanh[m][:], in_=score_bank[m][:], func=ACT.Tanh, scale=SCORE_SCALE)
+            if m == 0:
+                raw["tanh"] = raw_pool.tile([P, TILES, S], F32, tag="raw", name="tanh")
+            tanh[m] = raw["tanh"][:, m, :]
+            nc.scalar.activation(out=tanh[m], in_=score_bank[m][:], func=ACT.Tanh, scale=SCORE_SCALE)
             base[m] = keep.tile([P, S], F32, name="base_%d" % m)
             nc.vector.tensor_scalar(
                 out=base[m][:], in0=score_bank[m][:], scalar1=SCORE_SCALE, scalar2=None, op0=ALU.mult
@@ -197,10 +200,10 @@ def tile_chaoticattentionmechanism_pb_k_kernel(
 
         def bifurcate(m):
             nc.vector.scalar_tensor_tensor(
-                out=tanh[m][:], in0=tanh[m][:], scalar=1.0, in1=tanh[m][:], op0=ALU.subtract, op1=ALU.mult
+                out=tanh[m], in0=tanh[m], scalar=1.0, in1=tanh[m], op0=ALU.subtract, op1=ALU.mult
             )
             nc.vector.scalar_tensor_tensor(
-                out=base[m][:], in0=tanh[m][:], scalar=neg_bif[:, 0:1], in1=base[m][:], op0=ALU.mult, op1=ALU.add
+                out=base[m][:], in0=tanh[m], scalar=neg_bif[:, 0:1], in1=base[m][:], op0=ALU.mult, op1=ALU.add
             )
 
         def softmax_rows(m):
@@ -249,7 +252,7 @@ def tile_chaoticattentionmechanism_pb_k_kernel(
         def weigh_values(m, engines):
             inv_sum = stage.tile([P, 1], F32, tag="inv_sum")
             nc.vector.reciprocal(inv_sum[:], row_sum[m][:])
-            result = stage.tile([P, HALVES * S], F32, tag="result")
+            result = raw_pool.tile([P, HALVES * S], F32, tag="raw", name="result")
             for h in range(HALVES):
                 cols = slice(h * S, (h + 1) * S)
                 product = psum_work.tile([P, S], F32, tag="work", name="product")
@@ -296,9 +299,8 @@ def tile_chaoticattentionmechanism_pb_k_kernel(
 
         queue = []
         sent = 0
-        n_passes = FIRST_LATE * UNIT * PAIR
-        n_banks = n_main * UNIT
         first_pass_bank = 2 * UNIT
+        dense_banks = (2 * KEYS_FROM + 2) * UNIT
 
         def passes_of(n):
             return [(n, j, s) for j in range(UNIT) for s in range(PAIR)]
@@ -322,7 +324,7 @@ def tile_chaoticattentionmechanism_pb_k_kernel(
                 if c == 0 and n > 0 and units[n - 1][0] == "query":
                     queue.extend(passes_of(n - 1))
                 if done % RUN == 0:
-                    while sent < len(queue) and sent < (done - first_pass_bank) * n_passes // n_banks:
+                    while sent < len(queue) and sent < min(done, dense_banks) - first_pass_bank + max(0, done - dense_banks) * 2 // 3:
                         closed = multiply(*queue[sent])
                         sent += 1
                         if closed is not None:
@@ -337,21 +339,18 @@ def tile_chaoticattentionmechanism_pb_k_kernel(
             if VALUE_UNIT < n <= VALUE_UNIT + VALUE_PARTS:
                 quantise_values(n - VALUE_UNIT - 1)
 
-        queue.extend(passes_of(n_main - 1))
         for m in range(TILES + 1):
-            passes = queue[sent:] if m == 0 else passes_of(n_main + m - 1)
-            runs = UNIT // LATE_RUN
-            for run in range(runs):
+            for c in range(UNIT):
                 if m < TILES:
-                    for c in range(run * LATE_RUN, (run + 1) * LATE_RUN):
-                        transpose_piece(n_main + m, c, 0)
-                elif run == 0:
-                    quantise_queries(n_main + m - 1, 1)
-                if run == runs - 1 and m >= 3:
+                    transpose_piece(n_main + m, c, 0)
+            if m == TILES:
+                quantise_queries(n_main + m - 1, 1)
+            passes = queue[sent:] if m == 0 else passes_of(n_main + m - 1)
+            for index, item in enumerate(passes):
+                if m >= 3 and index == len(passes) // 2:
                     quantise_weights(m - 3)
                     weigh_values(m - 3, "SV")
-                for item in passes[run * len(passes) // runs : (run + 1) * len(passes) // runs]:
-                    multiply(*item)
+                multiply(*item)
             if m == 0:
                 continue
             if m >= 2:

@@ -35,9 +35,9 @@ PARTS = 2
 RUN = 4
 SCORE_SCALE = 1.0 / 32.0
 HALVES = 2
-VALUE_PARTS = 4
+VALUE_PARTS = 8
 VALUE_COLS = E // VALUE_PARTS
-VALUE_UNIT = 18
+VALUE_UNIT = 16
 BIFURCATE_UNIT = 6
 
 FLOPS = 2 * S * S * (E + 2 * HALF) + 2 * S * S * E
@@ -99,6 +99,9 @@ def tile_chaoticattentionmechanism_pb_k_kernel(
         weight_codes = {}
         weight_scales = {}
         grouped_values = {}
+        products = {}
+        inv_sum = {}
+        result = {}
 
         def new_raw():
             return raw_pool.tile([P, UNIT, PAIR_COLS], BF16, tag="raw", name="loaded")
@@ -149,8 +152,8 @@ def tile_chaoticattentionmechanism_pb_k_kernel(
 
         def quantise_keys(n):
             pair = units[n][1]
-            key_codes[pair] = keep.tile([P, PAIR * S], U32, name="key_codes_%d" % pair, align_bytes=256)
-            key_scales[pair] = keep.tile([P, PAIR * S], U8, name="key_scales_%d" % pair, align_bytes=256)
+            key_codes[pair] = keep.tile([P, PAIR * S], U32, name="key_codes_%d" % pair, align_bytes=64)
+            key_scales[pair] = keep.tile([P, PAIR * S], U8, name="key_scales_%d" % pair, align_bytes=64)
             nc.vector.quantize_mx(
                 out=key_codes[pair][:].bitcast(FP8X4), scales=key_scales[pair][:], in_=grouped[n][:]
             )
@@ -158,8 +161,8 @@ def tile_chaoticattentionmechanism_pb_k_kernel(
         def quantise_queries(n, part):
             n_words = UNIT * PAIR * P
             if part == 0:
-                query_codes[n] = stage.tile([P, n_words], U32, tag="query_codes", name="codes", bufs=3, align_bytes=256)
-                query_scales[n] = stage.tile([P, n_words], U8, tag="query_scales", name="scales", bufs=3, align_bytes=256)
+                query_codes[n] = stage.tile([P, n_words], U32, tag="query_codes", name="codes", bufs=3, align_bytes=64)
+                query_scales[n] = stage.tile([P, n_words], U8, tag="query_scales", name="scales", bufs=3, align_bytes=64)
             words = slice(part * n_words // PARTS, (part + 1) * n_words // PARTS)
             nc.vector.quantize_mx(
                 out=query_codes[n][:, words].bitcast(FP8X4),
@@ -199,9 +202,7 @@ def tile_chaoticattentionmechanism_pb_k_kernel(
             )
 
         def bifurcate(m):
-            nc.vector.scalar_tensor_tensor(
-                out=tanh[m], in0=tanh[m], scalar=1.0, in1=tanh[m], op0=ALU.subtract, op1=ALU.mult
-            )
+            nc.scalar.activation(out=tanh[m], in_=tanh[m], func=ACT.Square, bias=minus_half[:, 0:1], scale=1.0)
             nc.vector.scalar_tensor_tensor(
                 out=base[m][:], in0=tanh[m], scalar=neg_bif[:, 0:1], in1=base[m][:], op0=ALU.mult, op1=ALU.add
             )
@@ -249,13 +250,12 @@ def tile_chaoticattentionmechanism_pb_k_kernel(
                 in_=grouped_values[part][:].rearrange("p w j -> p (w j)"),
             )
 
-        def weigh_values(m, engines):
-            inv_sum = stage.tile([P, 1], F32, tag="inv_sum")
-            nc.vector.reciprocal(inv_sum[:], row_sum[m][:])
-            result = raw_pool.tile([P, HALVES * S], F32, tag="raw", name="result")
+        def weigh_values(m):
+            products[m] = []
             for h in range(HALVES):
                 cols = slice(h * S, (h + 1) * S)
                 product = psum_work.tile([P, S], F32, tag="work", name="product")
+                products[m].append(product)
                 nc.tensor.matmul_mx(
                     out=product[:],
                     lhsT=weight_codes[m][:].bitcast(FP8X4),
@@ -265,13 +265,23 @@ def tile_chaoticattentionmechanism_pb_k_kernel(
                     start=True,
                     stop=True,
                 )
-                if engines[h] == "S":
-                    nc.scalar.activation(out=result[:, cols], in_=product[:], func=ACT.Copy, scale=inv_sum[:, 0:1])
-                else:
-                    nc.vector.tensor_scalar(
-                        out=result[:, cols], in0=product[:], scalar1=inv_sum[:, 0:1], scalar2=None, op0=ALU.mult
-                    )
-                nc.sync.dma_start(out=out_rows[m][:, cols], in_=result[:, cols])
+
+        def invert_sum(m):
+            inv_sum[m] = keep.tile([P, 1], F32, name="inv_sum_%d" % m)
+            nc.vector.reciprocal(inv_sum[m][:], row_sum[m][:])
+            result[m] = raw_pool.tile([P, HALVES * S], F32, tag="raw", name="result")
+
+        def store(m, h, engine):
+            cols = slice(h * S, (h + 1) * S)
+            if engine == "S":
+                nc.scalar.activation(
+                    out=result[m][:, cols], in_=products[m][h][:], func=ACT.Copy, scale=inv_sum[m][:, 0:1]
+                )
+            else:
+                nc.vector.tensor_scalar(
+                    out=result[m][:, cols], in0=products[m][h][:], scalar1=inv_sum[m][:, 0:1], scalar2=None, op0=ALU.mult
+                )
+            nc.sync.dma_start(out=out_rows[m][:, cols], in_=result[m][:, cols])
 
         load_unit(0, UNIT)
         load_unit(1, UNIT)
@@ -290,6 +300,8 @@ def tile_chaoticattentionmechanism_pb_k_kernel(
         warm = keep.tile([P, 1], F32)
         nc.vector.memset(warm[:], 0.0)
         nc.scalar.activation(out=warm[:], in_=warm[:], func=ACT.Exp)
+        minus_half = keep.tile([P, 1], F32)
+        nc.vector.memset(minus_half[:], -0.5)
         neg_bif = keep.tile([P, 1], F32)
         nc.vector.tensor_scalar(out=neg_bif[:], in0=bif_raw[:], scalar1=-1.0, scalar2=None, op0=ALU.mult)
         coupling = keep.tile([P, 1], F32)
@@ -339,25 +351,44 @@ def tile_chaoticattentionmechanism_pb_k_kernel(
             if VALUE_UNIT < n <= VALUE_UNIT + VALUE_PARTS:
                 quantise_values(n - VALUE_UNIT - 1)
 
-        for m in range(TILES + 1):
+        for m in range(TILES):
             for c in range(UNIT):
-                if m < TILES:
-                    transpose_piece(n_main + m, c, 0)
-            if m == TILES:
-                quantise_queries(n_main + m - 1, 1)
+                transpose_piece(n_main + m, c, 0)
+            if m == TILES - 1:
+                quantise_weights(0)
+                quantise_queries(n_main + m, 1)
             passes = queue[sent:] if m == 0 else passes_of(n_main + m - 1)
             for index, item in enumerate(passes):
-                if m >= 3 and index == len(passes) // 2:
-                    quantise_weights(m - 3)
-                    weigh_values(m - 3, "SV")
+                if m == TILES - 1 and index == len(passes) - PAIR:
+                    weigh_values(0)
                 multiply(*item)
-            if m == 0:
-                continue
             if m >= 2:
                 transpose_weights(m - 2)
-            softmax_rows(m - 1)
-        quantise_weights(TILES - 2)
-        weigh_values(TILES - 2, "VV")
-        transpose_weights(TILES - 1)
-        quantise_weights(TILES - 1)
-        weigh_values(TILES - 1, "SV")
+            if m >= 1:
+                softmax_rows(m - 1)
+        invert_sum(0)
+        store(0, 0, "S")
+        store(0, 1, "S")
+
+        passes = passes_of(n_main + TILES - 1)
+        for index, item in enumerate(passes):
+            if index == len(passes) - PAIR:
+                quantise_weights(1)
+                weigh_values(1)
+            multiply(*item)
+        transpose_weights(2)
+        invert_sum(1)
+        store(1, 0, "S")
+        softmax_rows(3)
+        quantise_weights(2)
+        store(1, 1, "V")
+        transpose_weights(3)
+        weigh_values(2)
+        invert_sum(2)
+        store(2, 0, "S")
+        store(2, 1, "S")
+        quantise_weights(3)
+        invert_sum(3)
+        weigh_values(3)
+        store(3, 0, "S")
+        store(3, 1, "V")

from contextlib import ExitStack

import concourse.mybir as mybir
from concourse.masks import make_identity

F32 = mybir.dt.float32
BF16 = mybir.dt.bfloat16
U32 = mybir.dt.uint32
U8 = mybir.dt.uint8
FP8X4 = mybir.dt.float8_e4m3fn_x4
ALU = mybir.AluOpType
ACT = mybir.ActivationFunctionType

P = 128
PACK = 4
K_PASS = P * PACK
S = 512
TILES = S // P
E = 1024
HALF = 8192
WIDTHS = (E, HALF, HALF)
PAIR = 2
PAIR_COLS = PAIR * K_PASS
N_PAIRS = sum(WIDTHS) // PAIR_COLS
UNIT = 4
LATE_PAIRS = UNIT
FIRST_LATE = N_PAIRS - LATE_PAIRS
KEYS_FROM = FIRST_LATE - LATE_PAIRS
RAW_BUFS = 8
AHEAD = RAW_BUFS - 2
FIRST_FILLERS = 4
HEAD_FILLERS = 2
EMPTY = "VSSS"
PARTS = 2
RUN = 4
SCORE_SCALE = 1.0 / 32.0
HALVES = 2
VALUE_PARTS = 8
VALUE_COLS = E // VALUE_PARTS
VALUE_UNIT = 16
BIFURCATE_UNIT = 6

FLOPS = 2 * S * S * (E + 2 * HALF) + 2 * S * S * E


def tile_chaoticattentionmechanism_pb_k_kernel(
    tc, Q, K, V, cos_q, sin_q, cos_k, sin_k, bifurcation_param, phase_coupling, out
):
    nc = tc.nc
    with ExitStack() as ctx:
        ctx.enter_context(tc.manual_schedule())
        keep = ctx.enter_context(tc.tile_pool(name="keep", bufs=1))
        raw_pool = ctx.enter_context(tc.tile_pool(name="raw_pool", bufs=RAW_BUFS))
        stage = ctx.enter_context(tc.tile_pool(name="stage", bufs=2))
        psum_work = ctx.enter_context(tc.psum_pool(name="psum_work", bufs=4))
        psum_sync = ctx.enter_context(tc.psum_pool(name="psum_sync", bufs=TILES))

        query_rows = [
            a.rearrange("b s k -> (b s) k").rearrange("(m p) k -> p m k", p=P) for a in (Q, cos_q, sin_q)
        ]
        key_rows = [
            a.rearrange("b s k -> (b s) k").rearrange("(p t) k -> p t k", t=TILES) for a in (K, cos_k, sin_k)
        ]
        value_rows = V.rearrange("b s w -> (b s) w").rearrange("(p j) w -> p j w", j=PACK)
        out_rows = out.rearrange("b s w -> (b s) w").rearrange("(m p) w -> m p w", p=P)

        pairs = [(0, 0)]
        for array_index, n_far in ((1, 8), (2, 4)):
            for i in range(n_far // 2):
                for half in range(2):
                    pairs.append((array_index, (i + half * n_far // 2) * PAIR_COLS))
        pairs.extend([(2, (4 + i) * PAIR_COLS) for i in range(LATE_PAIRS)])

        units = []
        late = FIRST_LATE
        for pair in range(FIRST_LATE):
            units.append(("key", pair))
            units.append(("query", [(m, pair) for m in range(TILES)]))
            if pair >= KEYS_FROM:
                units.append(("key", late))
                late += 1
        n_main = len(units)
        for m in range(TILES):
            units.append(("query", [(m, pair) for pair in range(FIRST_LATE, N_PAIRS)]))

        raw = {}
        grouped = {}
        key_codes = {}
        key_scales = {}
        query_codes = {}
        query_scales = {}
        score_bank = {}
        sync_bank = {}
        tanh = {}
        base = {}
        weights = {}
        row_sum = {}
        grouped_weights = {}
        weight_codes = {}
        weight_scales = {}
        grouped_values = {}
        products = {}
        inv_sum = {}
        result = {}

        def new_raw():
            return raw_pool.tile([P, UNIT, PAIR_COLS], BF16, tag="raw", name="loaded")

        def load_unit(n, pieces):
            side, what = units[n]
            raw[n] = new_raw()
            if side == "key":
                array_index, col = pairs[what]
                source = key_rows[array_index][:, :, col : col + PAIR_COLS]
            else:
                m, pair = what[0]
                array_index, col = pairs[pair]
                if pair < FIRST_LATE:
                    source = query_rows[array_index][:, :, col : col + PAIR_COLS]
                else:
                    source = query_rows[array_index][:, m, col : col + UNIT * PAIR_COLS].rearrange(
                        "p (j k) -> p j k", j=UNIT
                    )
            step = UNIT // pieces
            for c in range(0, UNIT, step):
                nc.sync.dma_start(out=raw[n][:, c : c + step, :], in_=source[:, c : c + step, :])

        def transpose_bank(n, c, fillers):
            if c == 0:
                grouped[n] = stage.tile(
                    [P, UNIT * PAIR * P * PACK], BF16, tag="grouped_%s" % units[n][0], name="grouped", align_bytes=64
                )
            values = grouped[n][:].bitcast(F32)
            if units[n][0] == "key":
                view = values.rearrange("p (s t r u) -> p s t r u", s=PAIR, t=TILES, u=2)[:, :, c]
            else:
                view = values.rearrange("p (j s r u) -> p j s r u", j=UNIT, s=PAIR, u=2)[:, c]
            words = raw[n][:].bitcast(F32)
            bank = psum_work.tile([P, PAIR, 2, P], F32, tag="work", name="bank")
            for f in range(fillers):
                nc.tensor.matmul(
                    bank[:].rearrange("p s u r -> p (s u r)"), lhsT=zeros[:, 0:P], rhs=zeros[:], start=True, stop=True
                )
            for s in range(PAIR):
                for u in range(2):
                    w0 = (2 * s + u) * P
                    nc.tensor.transpose(bank[:, s, u, :], words[:, c, w0 : w0 + P], ident_f32[:])
            if EMPTY[c] == "S":
                nc.scalar.copy(out=view, in_=bank[:].rearrange("p s u r -> p s r u"))
            else:
                nc.vector.tensor_copy(out=view, in_=bank[:].rearrange("p s u r -> p s r u"))

        def quantise_keys(n):
            pair = units[n][1]
            key_codes[pair] = keep.tile([P, PAIR * S], U32, name="key_codes_%d" % pair, align_bytes=64)
            key_scales[pair] = keep.tile([P, PAIR * S], U8, name="key_scales_%d" % pair, align_bytes=64)
            nc.vector.quantize_mx(
                out=key_codes[pair][:].bitcast(FP8X4), scales=key_scales[pair][:], in_=grouped[n][:]
            )

        def quantise_queries(n, part):
            n_words = UNIT * PAIR * P
            if part == 0:
                query_codes[n] = stage.tile([P, n_words], U32, tag="query_codes", name="codes", bufs=3, align_bytes=64)
                query_scales[n] = stage.tile([P, n_words], U8, tag="query_scales", name="scales", bufs=3, align_bytes=64)
            words = slice(part * n_words // PARTS, (part + 1) * n_words // PARTS)
            nc.vector.quantize_mx(
                out=query_codes[n][:, words].bitcast(FP8X4),
                scales=query_scales[n][:, words],
                in_=grouped[n][:, words.start * PACK : words.stop * PACK],
            )

        def multiply(n, j, s):
            m, pair = units[n][1][j]
            opens = pair <= 1 and s == 0
            closes = pair in (0, N_PAIRS - 1) and s == PAIR - 1
            if opens and pair == 0:
                score_bank[m] = psum_sync.tile([P, S], F32, tag="sums", name="score_bank")
            if opens and pair == 1:
                sync_bank[m] = psum_sync.tile([P, S], F32, tag="sums", name="sync_bank")
            query_cols = slice((j * PAIR + s) * P, (j * PAIR + s + 1) * P)
            key_cols = slice(s * S, (s + 1) * S)
            nc.tensor.matmul_mx(
                out=(score_bank if pair == 0 else sync_bank)[m][:],
                lhsT=query_codes[n][:, query_cols].bitcast(FP8X4),
                lhsT_scale=query_scales[n][:, query_cols],
                rhs=key_codes[pair][:, key_cols].bitcast(FP8X4),
                rhs_scale=key_scales[pair][:, key_cols],
                start=opens,
                stop=closes,
            )
            return (m, pair) if closes else None

        def empty_scores(m):
            if m == 0:
                raw["tanh"] = raw_pool.tile([P, TILES, S], F32, tag="raw", name="tanh")
            tanh[m] = raw["tanh"][:, m, :]
            nc.scalar.activation(out=tanh[m], in_=score_bank[m][:], func=ACT.Tanh, scale=SCORE_SCALE)
            base[m] = keep.tile([P, S], F32, name="base_%d" % m)
            nc.vector.tensor_scalar(
                out=base[m][:], in0=score_bank[m][:], scalar1=SCORE_SCALE, scalar2=None, op0=ALU.mult
            )

        def bifurcate(m):
            nc.scalar.activation(out=tanh[m], in_=tanh[m], func=ACT.Square, bias=minus_half[:, 0:1], scale=1.0)
            nc.vector.scalar_tensor_tensor(
                out=base[m][:], in0=tanh[m], scalar=neg_bif[:, 0:1], in1=base[m][:], op0=ALU.mult, op1=ALU.add
            )

        def softmax_rows(m):
            nc.vector.scalar_tensor_tensor(
                out=base[m][:], in0=sync_bank[m][:], scalar=coupling[:, 0:1], in1=base[m][:], op0=ALU.mult, op1=ALU.add
            )
            neg_max = stage.tile([P, 1], F32, tag="neg_max")
            nc.vector.tensor_reduce(out=neg_max[:], in_=base[m][:], axis=mybir.AxisListType.X, op=ALU.max, negate=True)
            weights[m] = stage.tile([P, S], BF16, tag="weights", name="weights")
            row_sum[m] = keep.tile([P, 1], F32, name="row_sum_%d" % m)
            nc.scalar.activation(
                out=weights[m][:], in_=base[m][:], func=ACT.Exp, bias=neg_max[:, 0:1], scale=1.0, accum_out=row_sum[m][:]
            )

        def transpose_weights(m):
            flipped = psum_work.tile([P, TILES, P], BF16, tag="work", name="flipped")
            for t in range(TILES):
                nc.tensor.transpose(flipped[:, t, :], weights[m][:, t * P : (t + 1) * P], ident_bf16[:])
            grouped_weights[m] = stage.tile([P, P, PACK], BF16, tag="grouped_weights", name="grouped_weights", align_bytes=64)
            nc.scalar.copy(out=grouped_weights[m][:], in_=flipped[:].rearrange("p t q -> p q t"))

        def quantise_weights(m):
            weight_codes[m] = stage.tile([P, P], U32, tag="weight_codes", name="weight_codes", align_bytes=64)
            weight_scales[m] = stage.tile([P, P], U8, tag="weight_scales", name="weight_scales", align_bytes=64)
            nc.vector.quantize_mx(
                out=weight_codes[m][:].bitcast(FP8X4),
                scales=weight_scales[m][:],
                in_=grouped_weights[m][:].rearrange("p q t -> p (q t)"),
            )

        def regroup_values(part):
            cols = slice(part * VALUE_COLS, (part + 1) * VALUE_COLS)
            grouped_values[part] = stage.tile(
                [P, VALUE_COLS, PACK], BF16, tag="grouped_values", name="grouped_values", align_bytes=64
            )
            nc.scalar.copy(out=grouped_values[part][:], in_=raw["values"][:, :, cols].rearrange("p j w -> p w j"))

        def quantise_values(part):
            cols = slice(part * VALUE_COLS, (part + 1) * VALUE_COLS)
            nc.vector.quantize_mx(
                out=value_codes[:, cols].bitcast(FP8X4),
                scales=value_scales[:, cols],
                in_=grouped_values[part][:].rearrange("p w j -> p (w j)"),
            )

        def weigh_values(m):
            products[m] = []
            for h in range(HALVES):
                cols = slice(h * S, (h + 1) * S)
                product = psum_work.tile([P, S], F32, tag="work", name="product")
                products[m].append(product)
                nc.tensor.matmul_mx(
                    out=product[:],
                    lhsT=weight_codes[m][:].bitcast(FP8X4),
                    lhsT_scale=weight_scales[m][:],
                    rhs=value_codes[:, cols].bitcast(FP8X4),
                    rhs_scale=value_scales[:, cols],
                    start=True,
                    stop=True,
                )

        def invert_sum(m):
            inv_sum[m] = keep.tile([P, 1], F32, name="inv_sum_%d" % m)
            nc.vector.reciprocal(inv_sum[m][:], row_sum[m][:])
            result[m] = raw_pool.tile([P, HALVES * S], F32, tag="raw", name="result")

        def store(m, h, engine):
            cols = slice(h * S, (h + 1) * S)
            if engine == "S":
                nc.scalar.activation(
                    out=result[m][:, cols], in_=products[m][h][:], func=ACT.Copy, scale=inv_sum[m][:, 0:1]
                )
            else:
                nc.vector.tensor_scalar(
                    out=result[m][:, cols], in0=products[m][h][:], scalar1=inv_sum[m][:, 0:1], scalar2=None, op0=ALU.mult
                )
            nc.sync.dma_start(out=out_rows[m][:, cols], in_=result[m][:, cols])

        load_unit(0, UNIT)
        load_unit(1, UNIT)
        for n in range(2, AHEAD):
            load_unit(n, 2)
        bif_raw = keep.tile([P, 1], BF16)
        nc.scalar.dma_start(out=bif_raw[:], in_=bifurcation_param.partition_broadcast(P))
        coupling_raw = keep.tile([P, 1], BF16)
        nc.scalar.dma_start(out=coupling_raw[:], in_=phase_coupling.partition_broadcast(P))
        zeros = keep.tile([P, S], BF16)
        nc.vector.memset(zeros[:], 0.0)
        ident_f32 = keep.tile([P, P], F32)
        make_identity(nc, ident_f32[:])
        ident_bf16 = keep.tile([P, P], BF16)
        make_identity(nc, ident_bf16[:])
        warm = keep.tile([P, 1], F32)
        nc.vector.memset(warm[:], 0.0)
        nc.scalar.activation(out=warm[:], in_=warm[:], func=ACT.Exp)
        minus_half = keep.tile([P, 1], F32)
        nc.vector.memset(minus_half[:], -0.5)
        neg_bif = keep.tile([P, 1], F32)
        nc.vector.tensor_scalar(out=neg_bif[:], in0=bif_raw[:], scalar1=-1.0, scalar2=None, op0=ALU.mult)
        coupling = keep.tile([P, 1], F32)
        nc.vector.tensor_scalar(out=coupling[:], in0=coupling_raw[:], scalar1=1.0 / HALF, scalar2=None, op0=ALU.mult)
        value_codes = keep.tile([P, E], U32, align_bytes=64)
        value_scales = keep.tile([P, E], U8, align_bytes=64)

        queue = []
        sent = 0
        first_pass_bank = 2 * UNIT
        dense_banks = (2 * KEYS_FROM + 2) * UNIT

        def passes_of(n):
            return [(n, j, s) for j in range(UNIT) for s in range(PAIR)]

        def transpose_piece(n, c, fillers):
            if c == 0 and n + AHEAD < len(units):
                load_unit(n + AHEAD, 2)
            transpose_bank(n, c, fillers)
            if c == 0 and n > 0:
                if units[n - 1][0] == "key":
                    quantise_keys(n - 1)
                else:
                    quantise_queries(n - 1, 1)
            if c == 2 and units[n][0] == "query":
                quantise_queries(n, 0)

        for n in range(n_main):
            for c in range(UNIT):
                done = n * UNIT + c + 1
                transpose_piece(n, c, 0 if c > 0 or sent > 0 else FIRST_FILLERS if n == 0 else HEAD_FILLERS)
                if c == 0 and n > 0 and units[n - 1][0] == "query":
                    queue.extend(passes_of(n - 1))
                if done % RUN == 0:
                    while sent < len(queue) and sent < min(done, dense_banks) - first_pass_bank + max(0, done - dense_banks) * 2 // 3:
                        closed = multiply(*queue[sent])
                        sent += 1
                        if closed is not None:
                            empty_scores(closed[0])
            if n + AHEAD == VALUE_UNIT:
                raw["values"] = new_raw()
                nc.sync.dma_start(out=raw["values"][:], in_=value_rows)
            if BIFURCATE_UNIT <= n < BIFURCATE_UNIT + TILES:
                bifurcate(n - BIFURCATE_UNIT)
            if VALUE_UNIT <= n < VALUE_UNIT + VALUE_PARTS:
                regroup_values(n - VALUE_UNIT)
            if VALUE_UNIT < n <= VALUE_UNIT + VALUE_PARTS:
                quantise_values(n - VALUE_UNIT - 1)

        for m in range(TILES):
            for c in range(UNIT):
                transpose_piece(n_main + m, c, 0)
            if m == TILES - 1:
                quantise_weights(0)
                quantise_queries(n_main + m, 1)
            passes = queue[sent:] if m == 0 else passes_of(n_main + m - 1)
            for index, item in enumerate(passes):
                if m == TILES - 1 and index == len(passes) - PAIR:
                    weigh_values(0)
                multiply(*item)
            if m >= 2:
                transpose_weights(m - 2)
            if m >= 1:
                softmax_rows(m - 1)
        invert_sum(0)
        store(0, 0, "S")
        store(0, 1, "S")

        passes = passes_of(n_main + TILES - 1)
        for index, item in enumerate(passes):
            if index == len(passes) - PAIR:
                quantise_weights(1)
                weigh_values(1)
            multiply(*item)
        transpose_weights(2)
        invert_sum(1)
        store(1, 0, "S")
        softmax_rows(3)
        quantise_weights(2)
        store(1, 1, "V")
        transpose_weights(3)
        weigh_values(2)
        invert_sum(2)
        store(2, 0, "S")
        store(2, 1, "S")
        quantise_weights(3)
        invert_sum(3)
        weigh_values(3)
        store(3, 0, "S")
        store(3, 1, "V")
